import numpy as np
import ml_dtypes


def mxq(x, axis, fmt="e4m3"):
    dtype, down = {"e4m3": (ml_dtypes.float8_e4m3fn, 7), "e5m2": (ml_dtypes.float8_e5m2, 14)}[fmt]
    v = np.moveaxis(np.asarray(x, np.float32).astype(ml_dtypes.bfloat16).astype(np.float64), axis, -1)
    blocks = v.reshape(v.shape[:-1] + (-1, 32))
    amax = np.abs(blocks).max(-1, keepdims=True)
    byte = np.maximum(np.where(amax > 0, np.frexp(amax)[1] - 1 + 127, 0) - down, 1)
    scale = np.exp2(byte - 127.0)
    codes = (blocks / scale).astype(np.float32).astype(dtype).astype(np.float64)
    return np.moveaxis((codes * scale).reshape(v.shape), -1, axis)


WIDE = False


def mx_kscale(k):
    if not WIDE:
        return np.ones(k)
    levels = np.array([10, -10, 5, -5, 0])
    a = np.random.permutation(np.resize(levels, k // 512 * 4)).reshape(k // 512, 4)
    idx = np.arange(k)
    return np.exp2(a[idx // 512, idx % 128 // 32])


BF16 = ml_dtypes.bfloat16


def bf(x):
    return np.asarray(x, np.float32).astype(BF16)


def f64(x):
    return np.asarray(x).astype(np.float64)


B, I, H = 8192, 1024, 128


def sigmoid(v):
    return 1.0 / (1.0 + np.exp(-v))


def setup_inputs():
    s = mx_kscale(I)
    return {
        "input_": bf(np.random.standard_normal((B, I)) * s),
        "c_input": bf(np.random.standard_normal((B, 1, H))),
        "h_0": bf(np.random.standard_normal((B, H))),
        "weight_ih": bf(np.random.standard_normal((I, 3 * H)) / np.sqrt(I) / s[:, None]),
        "weight_hh": bf(np.random.standard_normal((H, 3 * H)) / np.sqrt(H)),
        "alpha_weight_ih": bf(np.random.standard_normal((I, H)) / np.sqrt(I) / s[:, None]),
        "alpha_weight_hh": bf(np.random.standard_normal((H, H)) / np.sqrt(H)),
        "bias": bf(np.random.standard_normal(3 * H) * 0.5),
        "alpha_bias": bf(np.random.standard_normal(H) * 0.5),
    }


def reference(input_, c_input, h_0, weight_ih, weight_hh, alpha_weight_ih, alpha_weight_hh, bias, alpha_bias):
    xq = mxq(f64(input_), 1, "e4m3")
    wh_b = f64(h_0) @ f64(weight_hh) + f64(bias)
    wi = xq @ mxq(f64(weight_ih), 0, "e4m3")
    pre = wh_b + wi
    i_gate = sigmoid(pre[:, :H])
    o_gate = sigmoid(pre[:, H:2 * H])
    g = np.tanh(pre[:, 2 * H:])
    c_in = f64(c_input)[:, 0, :]
    alpha = sigmoid((xq @ mxq(f64(alpha_weight_ih), 0, "e4m3")) + f64(alpha_bias) + c_in @ f64(alpha_weight_hh))
    e_i = np.exp(i_gate)
    e_a = np.exp(alpha)
    denom = e_i + e_a
    w_i = e_i / denom
    w_a = e_a / denom
    c_1 = w_i * g + w_a * c_in
    h_1 = o_gate * np.tanh(c_1)
    return (h_1, c_1)

@@ -1,0 +1,201 @@
+import concourse.mybir as mybir
+from concourse.masks import make_identity
+
+BF16 = mybir.dt.bfloat16
+F32 = mybir.dt.float32
+U32 = mybir.dt.uint32
+U8 = mybir.dt.uint8
+FP8X4 = mybir.dt.float8_e4m3fn_x4
+ACT = mybir.ActivationFunctionType
+ALU = mybir.AluOpType
+
+P = 128
+ROWS = 8192
+K = 1024
+H = 128
+GATES = 4 * H
+SIG = 3 * H
+PACK = 4
+K_PASS = P * PACK
+PASSES = K // K_PASS
+WORDS = K // 2
+TILES = ROWS // P
+GROUP = 4
+N_GROUPS = TILES // GROUP
+CHUNK = 4
+
+FLOPS = 2 * ROWS * (K + H) * GATES
+
+
+def tile_multiinputlstmcell_pa_t_kernel(
+    tc,
+    input_,
+    c_input,
+    h_0,
+    weight_ih,
+    weight_hh,
+    alpha_weight_ih,
+    alpha_weight_hh,
+    bias,
+    alpha_bias,
+    out_0,
+    out_1,
+):
+    nc = tc.nc
+
+    x_rows = input_.rearrange("(p n) k -> p n k", n=TILES)
+    h_rows = h_0.rearrange("(p n) h -> p (n h)", n=TILES)
+    c_rows = c_input.rearrange("(p n) o h -> p (n o h)", n=TILES)
+    h1_rows = out_0.rearrange("(p n) h -> p n h", n=TILES)
+    c1_rows = out_1.rearrange("(p n) h -> p n h", n=TILES)
+
+    with tc.tile_pool(name="consts", bufs=1) as consts, tc.tile_pool(
+        name="xin", bufs=3
+    ) as xin, tc.tile_pool(name="quant", bufs=2) as quant, tc.tile_pool(
+        name="work", bufs=2
+    ) as work, tc.psum_pool(name="psum_x", bufs=3) as psum_x, tc.psum_pool(
+        name="psum_hc", bufs=1
+    ) as psum_hc, tc.psum_pool(name="psum_plain", bufs=2) as psum_plain, tc.psum_pool(
+        name="psum_mx", bufs=2
+    ) as psum_mx:
+        ident_f32 = consts.tile([P, P], F32)
+        make_identity(nc, ident_f32[:])
+        ident_bf = consts.tile([P, P], BF16)
+        make_identity(nc, ident_bf[:])
+
+        w_raw = consts.tile([P, PASSES, PACK, SIG], BF16)
+        nc.scalar.dma_start(
+            out=w_raw[:].rearrange("p g (u e) c -> p (g u) (e c)", e=2),
+            in_=weight_ih.rearrange("(j p e) c -> p j (e c)", p=P, e=2),
+        )
+        a_raw = consts.tile([P, PASSES, PACK, H], BF16)
+        nc.scalar.dma_start(
+            out=a_raw[:].rearrange("p g (u e) c -> p (g u) (e c)", e=2),
+            in_=alpha_weight_ih.rearrange("(j p e) c -> p j (e c)", p=P, e=2),
+        )
+        whh = consts.tile([P, SIG], BF16)
+        nc.scalar.dma_start(out=whh[:], in_=weight_hh)
+        awhh = consts.tile([P, H], BF16)
+        nc.scalar.dma_start(out=awhh[:], in_=alpha_weight_hh)
+        bias_all = consts.tile([P, GATES], BF16)
+        nc.scalar.dma_start(out=bias_all[:, 0 : 2 * H], in_=bias[0 : 2 * H].partition_broadcast(P))
+        nc.scalar.dma_start(out=bias_all[:, 2 * H : SIG], in_=alpha_bias.partition_broadcast(P))
+        nc.scalar.dma_start(out=bias_all[:, SIG:GATES], in_=bias[2 * H : SIG].partition_broadcast(P))
+
+        w_grouped = consts.tile([P, PASSES, GATES, PACK], BF16, align_bytes=64)
+        w_codes = consts.tile([P, PASSES, GATES], U32, align_bytes=64)
+        w_scales = consts.tile([P, PASSES, GATES], U8, align_bytes=64)
+        for g in range(PASSES):
+            nc.vector.tensor_copy(
+                out=w_grouped[:, g, 0 : 2 * H, :],
+                in_=w_raw[:, g, :, 0 : 2 * H].rearrange("p t c -> p c t"),
+            )
+            nc.vector.tensor_copy(
+                out=w_grouped[:, g, 2 * H : SIG, :],
+                in_=a_raw[:, g, :, :].rearrange("p t c -> p c t"),
+            )
+            nc.vector.tensor_copy(
+                out=w_grouped[:, g, SIG:GATES, :],
+                in_=w_raw[:, g, :, 2 * H : SIG].rearrange("p t c -> p c t"),
+            )
+        for g in range(PASSES):
+            nc.vector.quantize_mx(
+                out=w_codes[:, g, :].bitcast(FP8X4),
+                scales=w_scales[:, g, :],
+                in_=w_grouped[:, g, :, :].rearrange("p c t -> p (c t)"),
+            )
+
+        h_sb = consts.tile([P, TILES * H], BF16)
+        c_sb = consts.tile([P, TILES * H], BF16)
+
+        for grp in range(N_GROUPS):
+            first = grp * GROUP
+
+            x_sb = xin.tile([P, GROUP, K], BF16)
+            nc.sync.dma_start(out=x_sb[:], in_=x_rows[:, first : first + GROUP, :])
+            if grp % CHUNK == 0:
+                cols = slice(first * H, (first + CHUNK * GROUP) * H)
+                nc.sync.dma_start(out=h_sb[:, cols], in_=h_rows[:, cols])
+                nc.sync.dma_start(out=c_sb[:, cols], in_=c_rows[:, cols])
+
+            x_words = x_sb[:].rearrange("p n k -> p (n k)").bitcast(F32)
+            x_grouped = quant.tile([P, GROUP * K], BF16, align_bytes=64)
+            grouped_words = x_grouped[:].bitcast(F32)
+            for t in range(GROUP):
+                x_t = psum_x.tile([P, 2 * PASSES, P], F32)
+                for j in range(2 * PASSES):
+                    lo = t * WORDS + j * P
+                    nc.tensor.transpose(x_t[:, j, :], x_words[:, lo : lo + P], ident_f32[:])
+                nc.scalar.copy(
+                    out=grouped_words[:, t * WORDS : (t + 1) * WORDS].rearrange(
+                        "p (g r u) -> p g r u", g=PASSES, u=2
+                    ),
+                    in_=x_t[:].rearrange("p (g u) r -> p g r u", u=2),
+                )
+            x_codes = quant.tile([P, GROUP * PASSES * P], U32, align_bytes=64)
+            x_scales = quant.tile([P, GROUP * PASSES * P], U8, align_bytes=64)
+            nc.vector.quantize_mx(
+                out=x_codes[:].bitcast(FP8X4), scales=x_scales[:], in_=x_grouped[:]
+            )
+
+            hc_ps = psum_hc.tile([P, 2 * GROUP, P], BF16)
+            for t in range(GROUP):
+                cols = slice((first + t) * H, (first + t + 1) * H)
+                nc.tensor.transpose(hc_ps[:, t, :], h_sb[:, cols], ident_bf[:])
+                nc.tensor.transpose(hc_ps[:, GROUP + t, :], c_sb[:, cols], ident_bf[:])
+            hc_t = work.tile([P, 2 * GROUP, P], BF16)
+            nc.scalar.copy(out=hc_t[:], in_=hc_ps[:])
+
+            pre = work.tile([P, GROUP, GATES], F32)
+            for t in range(GROUP):
+                plain = psum_plain.tile([P, GATES], F32)
+                nc.tensor.matmul(
+                    plain[:, 0 : 2 * H], lhsT=hc_t[:, t, :], rhs=whh[:, 0 : 2 * H], start=True, stop=True
+                )
+                nc.tensor.matmul(
+                    plain[:, 2 * H : SIG], lhsT=hc_t[:, GROUP + t, :], rhs=awhh[:], start=True, stop=True
+                )
+                nc.tensor.matmul(
+                    plain[:, SIG:GATES], lhsT=hc_t[:, t, :], rhs=whh[:, 2 * H : SIG], start=True, stop=True
+                )
+                nc.vector.tensor_tensor(out=pre[:, t, :], in0=plain[:], in1=bias_all[:], op=ALU.add)
+            for t in range(GROUP):
+                acc = psum_mx.tile([P, GATES], F32)
+                for g in range(PASSES):
+                    lo = (t * PASSES + g) * P
+                    nc.tensor.matmul_mx(
+                        out=acc[:],
+                        lhsT=x_codes[:, lo : lo + P].bitcast(FP8X4),
+                        lhsT_scale=x_scales[:, lo : lo + P],
+                        rhs=w_codes[:, g, :].bitcast(FP8X4),
+                        rhs_scale=w_scales[:, g, :],
+                        start=(g == 0),
+                        stop=(g == PASSES - 1),
+                    )
+                nc.vector.tensor_tensor(out=pre[:, t, :], in0=acc[:], in1=pre[:, t, :], op=ALU.add)
+
+            gates = work.tile([P, GROUP, GATES], F32)
+            nc.scalar.activation(out=gates[:, :, 0:SIG], in_=pre[:, :, 0:SIG], func=ACT.Sigmoid)
+            nc.scalar.activation(out=gates[:, :, SIG:GATES], in_=pre[:, :, SIG:GATES], func=ACT.Tanh)
+            i_gate = gates[:, :, 0:H]
+            o_gate = gates[:, :, H : 2 * H]
+            alpha = gates[:, :, 2 * H : SIG]
+            g_gate = gates[:, :, SIG:GATES]
+            c_in = c_sb[:, first * H : (first + GROUP) * H].rearrange("p (n h) -> p n h", h=H)
+
+            diff = work.tile([P, GROUP, H], F32)
+            nc.vector.tensor_tensor(out=diff[:], in0=i_gate, in1=alpha, op=ALU.subtract)
+            w_i = work.tile([P, GROUP, H], F32)
+            nc.scalar.activation(out=w_i[:], in_=diff[:], func=ACT.Sigmoid)
+            move = work.tile([P, GROUP, H], F32)
+            nc.vector.tensor_tensor(out=move[:], in0=g_gate, in1=c_in, op=ALU.subtract)
+            step = work.tile([P, GROUP, H], F32)
+            nc.vector.tensor_tensor(out=step[:], in0=w_i[:], in1=move[:], op=ALU.mult)
+            c_1 = work.tile([P, GROUP, H], F32)
+            nc.vector.tensor_tensor(out=c_1[:], in0=step[:], in1=c_in, op=ALU.add)
+            nc.sync.dma_start(out=c1_rows[:, first : first + GROUP, :], in_=c_1[:])
+            tanh_c = work.tile([P, GROUP, H], F32)
+            nc.scalar.activation(out=tanh_c[:], in_=c_1[:], func=ACT.Tanh)
+            h_1 = work.tile([P, GROUP, H], F32)
+            nc.vector.tensor_tensor(out=h_1[:], in0=o_gate, in1=tanh_c[:], op=ALU.mult)
+            nc.sync.dma_start(out=h1_rows[:, first : first + GROUP, :], in_=h_1[:])

@@ -188,14 +188,14 @@ def tile_multiinputlstmcell_pa_t_kernel(
             w_i = work.tile([P, GROUP, H], F32)
             nc.scalar.activation(out=w_i[:], in_=diff[:], func=ACT.Sigmoid)
             move = work.tile([P, GROUP, H], F32)
-            nc.vector.tensor_tensor(out=move[:], in0=g_gate, in1=c_in, op=ALU.subtract)
+            nc.gpsimd.tensor_tensor(out=move[:], in0=g_gate, in1=c_in, op=ALU.subtract)
             step = work.tile([P, GROUP, H], F32)
-            nc.vector.tensor_tensor(out=step[:], in0=w_i[:], in1=move[:], op=ALU.mult)
+            nc.gpsimd.tensor_tensor(out=step[:], in0=w_i[:], in1=move[:], op=ALU.mult)
             c_1 = work.tile([P, GROUP, H], F32)
-            nc.vector.tensor_tensor(out=c_1[:], in0=step[:], in1=c_in, op=ALU.add)
+            nc.gpsimd.tensor_tensor(out=c_1[:], in0=step[:], in1=c_in, op=ALU.add)
             nc.sync.dma_start(out=c1_rows[:, first : first + GROUP, :], in_=c_1[:])
             tanh_c = work.tile([P, GROUP, H], F32)
             nc.scalar.activation(out=tanh_c[:], in_=c_1[:], func=ACT.Tanh)
             h_1 = work.tile([P, GROUP, H], F32)
-            nc.vector.tensor_tensor(out=h_1[:], in0=o_gate, in1=tanh_c[:], op=ALU.mult)
+            nc.gpsimd.tensor_tensor(out=h_1[:], in0=o_gate, in1=tanh_c[:], op=ALU.mult)
             nc.sync.dma_start(out=h1_rows[:, first : first + GROUP, :], in_=h_1[:])

@@ -51,9 +51,9 @@ def tile_multiinputlstmcell_pa_t_kernel(
 
     with tc.tile_pool(name="consts", bufs=1) as consts, tc.tile_pool(
         name="xin", bufs=3
-    ) as xin, tc.tile_pool(name="quant", bufs=2) as quant, tc.tile_pool(
-        name="work", bufs=2
-    ) as work, tc.psum_pool(name="psum_x", bufs=3) as psum_x, tc.psum_pool(
+    ) as xin, tc.tile_pool(name="two", bufs=2) as two, tc.tile_pool(
+        name="four", bufs=4
+    ) as four, tc.psum_pool(name="psum_x", bufs=3) as psum_x, tc.psum_pool(
         name="psum_hc", bufs=1
     ) as psum_hc, tc.psum_pool(name="psum_plain", bufs=2) as psum_plain, tc.psum_pool(
         name="psum_mx", bufs=2
@@ -108,18 +108,27 @@ def tile_multiinputlstmcell_pa_t_kernel(
         h_sb = consts.tile([P, TILES * H], BF16)
         c_sb = consts.tile([P, TILES * H], BF16)
 
-        for grp in range(N_GROUPS):
-            first = grp * GROUP
+        x_in, x_side, x_code, x_scale, hc_side = {}, {}, {}, {}, {}
+        pre_of, gates_of, diff_of, w_of, move_of, step_of, c1_of, tanh_of = {}, {}, {}, {}, {}, {}, {}, {}
 
+        def c_in_of(grp):
+            lo = grp * GROUP * H
+            return c_sb[:, lo : lo + GROUP * H].rearrange("p (n h) -> p n h", h=H)
+
+        def load(grp):
+            first = grp * GROUP
             x_sb = xin.tile([P, GROUP, K], BF16)
             nc.sync.dma_start(out=x_sb[:], in_=x_rows[:, first : first + GROUP, :])
+            x_in[grp] = x_sb
             if grp % CHUNK == 0:
                 cols = slice(first * H, (first + CHUNK * GROUP) * H)
                 nc.sync.dma_start(out=h_sb[:, cols], in_=h_rows[:, cols])
                 nc.sync.dma_start(out=c_sb[:, cols], in_=c_rows[:, cols])
 
-            x_words = x_sb[:].rearrange("p n k -> p (n k)").bitcast(F32)
-            x_grouped = quant.tile([P, GROUP * K], BF16, align_bytes=64)
+        def transpose(grp):
+            first = grp * GROUP
+            x_words = x_in[grp][:].rearrange("p n k -> p (n k)").bitcast(F32)
+            x_grouped = two.tile([P, GROUP * K], BF16, align_bytes=64)
             grouped_words = x_grouped[:].bitcast(F32)
             for t in range(GROUP):
                 x_t = psum_x.tile([P, 2 * PASSES, P], F32)
@@ -132,70 +141,130 @@ def tile_multiinputlstmcell_pa_t_kernel(
                     ),
                     in_=x_t[:].rearrange("p (g u) r -> p g r u", u=2),
                 )
-            x_codes = quant.tile([P, GROUP * PASSES * P], U32, align_bytes=64)
-            x_scales = quant.tile([P, GROUP * PASSES * P], U8, align_bytes=64)
-            nc.vector.quantize_mx(
-                out=x_codes[:].bitcast(FP8X4), scales=x_scales[:], in_=x_grouped[:]
-            )
-
+            x_side[grp] = x_grouped
             hc_ps = psum_hc.tile([P, 2 * GROUP, P], BF16)
             for t in range(GROUP):
                 cols = slice((first + t) * H, (first + t + 1) * H)
                 nc.tensor.transpose(hc_ps[:, t, :], h_sb[:, cols], ident_bf[:])
                 nc.tensor.transpose(hc_ps[:, GROUP + t, :], c_sb[:, cols], ident_bf[:])
-            hc_t = work.tile([P, 2 * GROUP, P], BF16)
+            hc_t = two.tile([P, 2 * GROUP, P], BF16)
             nc.scalar.copy(out=hc_t[:], in_=hc_ps[:])
+            hc_side[grp] = hc_t
 
-            pre = work.tile([P, GROUP, GATES], F32)
-            for t in range(GROUP):
-                plain = psum_plain.tile([P, GATES], F32)
-                nc.tensor.matmul(
-                    plain[:, 0 : 2 * H], lhsT=hc_t[:, t, :], rhs=whh[:, 0 : 2 * H], start=True, stop=True
-                )
-                nc.tensor.matmul(
-                    plain[:, 2 * H : SIG], lhsT=hc_t[:, GROUP + t, :], rhs=awhh[:], start=True, stop=True
-                )
-                nc.tensor.matmul(
-                    plain[:, SIG:GATES], lhsT=hc_t[:, t, :], rhs=whh[:, 2 * H : SIG], start=True, stop=True
-                )
-                nc.vector.tensor_tensor(out=pre[:, t, :], in0=plain[:], in1=bias_all[:], op=ALU.add)
-            for t in range(GROUP):
-                acc = psum_mx.tile([P, GATES], F32)
-                for g in range(PASSES):
-                    lo = (t * PASSES + g) * P
-                    nc.tensor.matmul_mx(
-                        out=acc[:],
-                        lhsT=x_codes[:, lo : lo + P].bitcast(FP8X4),
-                        lhsT_scale=x_scales[:, lo : lo + P],
-                        rhs=w_codes[:, g, :].bitcast(FP8X4),
-                        rhs_scale=w_scales[:, g, :],
-                        start=(g == 0),
-                        stop=(g == PASSES - 1),
-                    )
-                nc.vector.tensor_tensor(out=pre[:, t, :], in0=acc[:], in1=pre[:, t, :], op=ALU.add)
+        def quantise(grp):
+            x_codes = two.tile([P, GROUP * PASSES * P], U32, align_bytes=64)
+            x_scales = two.tile([P, GROUP * PASSES * P], U8, align_bytes=64)
+            nc.vector.quantize_mx(
+                out=x_codes[:].bitcast(FP8X4), scales=x_scales[:], in_=x_side[grp][:]
+            )
+            x_code[grp] = x_codes
+            x_scale[grp] = x_scales
 
-            gates = work.tile([P, GROUP, GATES], F32)
+        def plain_product(grp, t, pre):
+            hc_t = hc_side[grp]
+            plain = psum_plain.tile([P, GATES], F32)
+            nc.tensor.matmul(
+                plain[:, 0 : 2 * H], lhsT=hc_t[:, t, :], rhs=whh[:, 0 : 2 * H], start=True, stop=True
+            )
+            nc.tensor.matmul(
+                plain[:, 2 * H : SIG], lhsT=hc_t[:, GROUP + t, :], rhs=awhh[:], start=True, stop=True
+            )
+            nc.tensor.matmul(
+                plain[:, SIG:GATES], lhsT=hc_t[:, t, :], rhs=whh[:, 2 * H : SIG], start=True, stop=True
+            )
+            nc.vector.tensor_tensor(out=pre[:, t, :], in0=plain[:], in1=bias_all[:], op=ALU.add)
+
+        def mx_product(grp, t, pre):
+            acc = psum_mx.tile([P, GATES], F32)
+            for g in range(PASSES):
+                lo = (t * PASSES + g) * P
+                nc.tensor.matmul_mx(
+                    out=acc[:],
+                    lhsT=x_code[grp][:, lo : lo + P].bitcast(FP8X4),
+                    lhsT_scale=x_scale[grp][:, lo : lo + P],
+                    rhs=w_codes[:, g, :].bitcast(FP8X4),
+                    rhs_scale=w_scales[:, g, :],
+                    start=(g == 0),
+                    stop=(g == PASSES - 1),
+                )
+            nc.vector.tensor_tensor(out=pre[:, t, :], in0=acc[:], in1=pre[:, t, :], op=ALU.add)
+
+        def products(grp):
+            pre = two.tile([P, GROUP, GATES], F32)
+            for t in range(GROUP + 1):
+                if t < GROUP:
+                    plain_product(grp, t, pre)
+                if t > 0:
+                    mx_product(grp, t - 1, pre)
+            pre_of[grp] = pre
+
+        def activate(grp):
+            pre = pre_of[grp]
+            gates = four.tile([P, GROUP, GATES], F32)
             nc.scalar.activation(out=gates[:, :, 0:SIG], in_=pre[:, :, 0:SIG], func=ACT.Sigmoid)
             nc.scalar.activation(out=gates[:, :, SIG:GATES], in_=pre[:, :, SIG:GATES], func=ACT.Tanh)
-            i_gate = gates[:, :, 0:H]
-            o_gate = gates[:, :, H : 2 * H]
-            alpha = gates[:, :, 2 * H : SIG]
-            g_gate = gates[:, :, SIG:GATES]
-            c_in = c_sb[:, first * H : (first + GROUP) * H].rearrange("p (n h) -> p n h", h=H)
+            gates_of[grp] = gates
 
-            diff = work.tile([P, GROUP, H], F32)
-            nc.vector.tensor_tensor(out=diff[:], in0=i_gate, in1=alpha, op=ALU.subtract)
-            w_i = work.tile([P, GROUP, H], F32)
-            nc.scalar.activation(out=w_i[:], in_=diff[:], func=ACT.Sigmoid)
-            move = work.tile([P, GROUP, H], F32)
-            nc.gpsimd.tensor_tensor(out=move[:], in0=g_gate, in1=c_in, op=ALU.subtract)
-            step = work.tile([P, GROUP, H], F32)
-            nc.gpsimd.tensor_tensor(out=step[:], in0=w_i[:], in1=move[:], op=ALU.mult)
-            c_1 = work.tile([P, GROUP, H], F32)
-            nc.gpsimd.tensor_tensor(out=c_1[:], in0=step[:], in1=c_in, op=ALU.add)
+        def gate_difference(grp):
+            gates = gates_of[grp]
+            diff = two.tile([P, GROUP, H], F32)
+            nc.vector.tensor_tensor(
+                out=diff[:], in0=gates[:, :, 0:H], in1=gates[:, :, 2 * H : SIG], op=ALU.subtract
+            )
+            diff_of[grp] = diff
+
+        def pair_weight(grp):
+            w_i = two.tile([P, GROUP, H], F32)
+            nc.scalar.activation(out=w_i[:], in_=diff_of[grp][:], func=ACT.Sigmoid)
+            w_of[grp] = w_i
+
+        def g_minus_c(grp):
+            move = two.tile([P, GROUP, H], F32)
+            nc.gpsimd.tensor_tensor(
+                out=move[:], in0=gates_of[grp][:, :, SIG:GATES], in1=c_in_of(grp), op=ALU.subtract
+            )
+            move_of[grp] = move
+
+        def weighted_move(grp):
+            step = two.tile([P, GROUP, H], F32)
+            nc.gpsimd.tensor_tensor(out=step[:], in0=w_of[grp][:], in1=move_of[grp][:], op=ALU.mult)
+            step_of[grp] = step
+
+        def new_cell(grp):
+            first = grp * GROUP
+            c_1 = two.tile([P, GROUP, H], F32)
+            nc.gpsimd.tensor_tensor(out=c_1[:], in0=step_of[grp][:], in1=c_in_of(grp), op=ALU.add)
             nc.sync.dma_start(out=c1_rows[:, first : first + GROUP, :], in_=c_1[:])
-            tanh_c = work.tile([P, GROUP, H], F32)
-            nc.scalar.activation(out=tanh_c[:], in_=c_1[:], func=ACT.Tanh)
-            h_1 = work.tile([P, GROUP, H], F32)
-            nc.gpsimd.tensor_tensor(out=h_1[:], in0=o_gate, in1=tanh_c[:], op=ALU.mult)
+            c1_of[grp] = c_1
+
+        def tanh_cell(grp):
+            tanh_c = two.tile([P, GROUP, H], F32)
+            nc.scalar.activation(out=tanh_c[:], in_=c1_of[grp][:], func=ACT.Tanh)
+            tanh_of[grp] = tanh_c
+
+        def new_hidden(grp):
+            first = grp * GROUP
+            h_1 = two.tile([P, GROUP, H], F32)
+            nc.gpsimd.tensor_tensor(
+                out=h_1[:], in0=gates_of[grp][:, :, H : 2 * H], in1=tanh_of[grp][:], op=ALU.mult
+            )
             nc.sync.dma_start(out=h1_rows[:, first : first + GROUP, :], in_=h_1[:])
+
+        def run(stage, grp):
+            if 0 <= grp < N_GROUPS:
+                stage(grp)
+
+        with tc.manual_schedule():
+            for rnd in range(-3, N_GROUPS + 4):
+                run(load, rnd + 3)
+                run(activate, rnd - 1)
+                run(pair_weight, rnd - 2)
+                run(weighted_move, rnd - 3)
+                run(g_minus_c, rnd - 2)
+                run(new_cell, rnd - 3)
+                run(new_hidden, rnd - 4)
+                run(products, rnd)
+                run(transpose, rnd + 2)
+                run(quantise, rnd + 1)
+                run(gate_difference, rnd - 1)
+                run(tanh_cell, rnd - 3)

@@ -20,9 +20,9 @@ K_PASS = P * PACK
 PASSES = K // K_PASS
 WORDS = K // 2
 TILES = ROWS // P
-GROUP = 4
+GROUP = 2
 N_GROUPS = TILES // GROUP
-CHUNK = 4
+CHUNK = 8
 
 FLOPS = 2 * ROWS * (K + H) * GATES
 

@@ -20,9 +20,10 @@ K_PASS = P * PACK
 PASSES = K // K_PASS
 WORDS = K // 2
 TILES = ROWS // P
-GROUP = 2
+GROUP = 4
 N_GROUPS = TILES // GROUP
-CHUNK = 8
+CHUNK = 2
+LEAD = 1
 
 FLOPS = 2 * ROWS * (K + H) * GATES
 
@@ -50,83 +51,113 @@ def tile_multiinputlstmcell_pa_t_kernel(
     c1_rows = out_1.rearrange("(p n) h -> p n h", n=TILES)
 
     with tc.tile_pool(name="consts", bufs=1) as consts, tc.tile_pool(
-        name="xin", bufs=3
-    ) as xin, tc.tile_pool(name="two", bufs=2) as two, tc.tile_pool(
-        name="four", bufs=4
-    ) as four, tc.psum_pool(name="psum_x", bufs=3) as psum_x, tc.psum_pool(
-        name="psum_hc", bufs=1
-    ) as psum_hc, tc.psum_pool(name="psum_plain", bufs=2) as psum_plain, tc.psum_pool(
-        name="psum_mx", bufs=2
-    ) as psum_mx:
+        name="two", bufs=2
+    ) as two, tc.tile_pool(name="x_pool", bufs=3) as x_pool, tc.tile_pool(
+        name="gates_pool", bufs=4
+    ) as gates_pool, tc.tile_pool(name="pre_pool", bufs=LEAD + 2) as pre_pool, tc.psum_pool(
+        name="psum_x", bufs=3
+    ) as psum_x, tc.psum_pool(name="psum_hc", bufs=1) as psum_hc, tc.psum_pool(
+        name="psum_plain", bufs=2
+    ) as psum_plain, tc.psum_pool(name="psum_mx", bufs=2) as psum_mx:
+        warm = consts.tile([P, 1], F32)
+        nc.vector.memset(warm[:], 0.0)
+        nc.scalar.activation(out=warm[:], in_=warm[:], func=ACT.Sigmoid)
+
+        whh = consts.tile([P, SIG], BF16)
+        nc.scalar.dma_start(out=whh[:], in_=weight_hh)
+        awhh = consts.tile([P, H], BF16)
+        nc.scalar.dma_start(out=awhh[:], in_=alpha_weight_hh)
+
+        bias_row = consts.tile([P, GATES], BF16)
+        nc.vector.memset(bias_row[:], 0.0)
+        nc.scalar.dma_start(out=bias_row[0:1, 0 : 2 * H], in_=bias[0 : 2 * H].unsqueeze(0))
+        nc.scalar.dma_start(out=bias_row[0:1, 2 * H : SIG], in_=alpha_bias.unsqueeze(0))
+        nc.scalar.dma_start(out=bias_row[0:1, SIG:GATES], in_=bias[2 * H : SIG].unsqueeze(0))
+        ones = consts.tile([P, P], BF16)
+        nc.vector.memset(ones[:], 1.0)
+        bias_ps = psum_plain.tile([P, GATES], F32, tag="plain")
+        nc.tensor.matmul(bias_ps[:], lhsT=ones[:], rhs=bias_row[:], start=True, stop=True)
+        bias_all = consts.tile([P, GATES], F32)
+        nc.vector.tensor_copy(out=bias_all[:], in_=bias_ps[:])
+
         ident_f32 = consts.tile([P, P], F32)
         make_identity(nc, ident_f32[:])
         ident_bf = consts.tile([P, P], BF16)
         make_identity(nc, ident_bf[:])
 
         w_raw = consts.tile([P, PASSES, PACK, SIG], BF16)
-        nc.scalar.dma_start(
-            out=w_raw[:].rearrange("p g (u e) c -> p (g u) (e c)", e=2),
-            in_=weight_ih.rearrange("(j p e) c -> p j (e c)", p=P, e=2),
-        )
         a_raw = consts.tile([P, PASSES, PACK, H], BF16)
-        nc.scalar.dma_start(
-            out=a_raw[:].rearrange("p g (u e) c -> p (g u) (e c)", e=2),
-            in_=alpha_weight_ih.rearrange("(j p e) c -> p j (e c)", p=P, e=2),
-        )
-        whh = consts.tile([P, SIG], BF16)
-        nc.scalar.dma_start(out=whh[:], in_=weight_hh)
-        awhh = consts.tile([P, H], BF16)
-        nc.scalar.dma_start(out=awhh[:], in_=alpha_weight_hh)
-        bias_all = consts.tile([P, GATES], BF16)
-        nc.scalar.dma_start(out=bias_all[:, 0 : 2 * H], in_=bias[0 : 2 * H].partition_broadcast(P))
-        nc.scalar.dma_start(out=bias_all[:, 2 * H : SIG], in_=alpha_bias.partition_broadcast(P))
-        nc.scalar.dma_start(out=bias_all[:, SIG:GATES], in_=bias[2 * H : SIG].partition_broadcast(P))
-
         w_grouped = consts.tile([P, PASSES, GATES, PACK], BF16, align_bytes=64)
         w_codes = consts.tile([P, PASSES, GATES], U32, align_bytes=64)
         w_scales = consts.tile([P, PASSES, GATES], U8, align_bytes=64)
-        for g in range(PASSES):
-            nc.vector.tensor_copy(
-                out=w_grouped[:, g, 0 : 2 * H, :],
-                in_=w_raw[:, g, :, 0 : 2 * H].rearrange("p t c -> p c t"),
-            )
-            nc.vector.tensor_copy(
-                out=w_grouped[:, g, 2 * H : SIG, :],
-                in_=a_raw[:, g, :, :].rearrange("p t c -> p c t"),
-            )
-            nc.vector.tensor_copy(
-                out=w_grouped[:, g, SIG:GATES, :],
-                in_=w_raw[:, g, :, 2 * H : SIG].rearrange("p t c -> p c t"),
-            )
-        for g in range(PASSES):
-            nc.vector.quantize_mx(
-                out=w_codes[:, g, :].bitcast(FP8X4),
-                scales=w_scales[:, g, :],
-                in_=w_grouped[:, g, :, :].rearrange("p c t -> p (c t)"),
-            )
-
         h_sb = consts.tile([P, TILES * H], BF16)
         c_sb = consts.tile([P, TILES * H], BF16)
 
+        def load_weights():
+            nc.sync.dma_start(
+                out=w_raw[:].rearrange("p g (u e) c -> p (g u) (e c)", e=2),
+                in_=weight_ih.rearrange("(j p e) c -> p j (e c)", p=P, e=2),
+            )
+            nc.sync.dma_start(
+                out=a_raw[:].rearrange("p g (u e) c -> p (g u) (e c)", e=2),
+                in_=alpha_weight_ih.rearrange("(j p e) c -> p j (e c)", p=P, e=2),
+            )
+
+        def regroup_weights():
+            for g in range(PASSES):
+                nc.vector.tensor_copy(
+                    out=w_grouped[:, g, 0 : 2 * H, :],
+                    in_=w_raw[:, g, :, 0 : 2 * H].rearrange("p t c -> p c t"),
+                )
+                nc.vector.tensor_copy(
+                    out=w_grouped[:, g, SIG:GATES, :],
+                    in_=w_raw[:, g, :, 2 * H : SIG].rearrange("p t c -> p c t"),
+                )
+                nc.vector.tensor_copy(
+                    out=w_grouped[:, g, 2 * H : SIG, :],
+                    in_=a_raw[:, g, :, :].rearrange("p t c -> p c t"),
+                )
+
+        def quantise_weights():
+            for g in range(PASSES):
+                nc.vector.quantize_mx(
+                    out=w_codes[:, g, :].bitcast(FP8X4),
+                    scales=w_scales[:, g, :],
+                    in_=w_grouped[:, g, :, :].rearrange("p c t -> p (c t)"),
+                )
+
         x_in, x_side, x_code, x_scale, hc_side = {}, {}, {}, {}, {}
         pre_of, gates_of, diff_of, w_of, move_of, step_of, c1_of, tanh_of = {}, {}, {}, {}, {}, {}, {}, {}
+
+        def rows_of(grp):
+            return slice(grp * GROUP, (grp + 1) * GROUP)
 
         def c_in_of(grp):
             lo = grp * GROUP * H
             return c_sb[:, lo : lo + GROUP * H].rearrange("p (n h) -> p n h", h=H)
 
-        def load(grp):
-            first = grp * GROUP
-            x_sb = xin.tile([P, GROUP, K], BF16)
-            nc.sync.dma_start(out=x_sb[:], in_=x_rows[:, first : first + GROUP, :])
+        def load_x(grp):
+            x_sb = x_pool.tile([P, GROUP, K], BF16)
+            nc.sync.dma_start(out=x_sb[:], in_=x_rows[:, rows_of(grp), :])
             x_in[grp] = x_sb
+
+        def load_state(grp):
             if grp % CHUNK == 0:
-                cols = slice(first * H, (first + CHUNK * GROUP) * H)
+                cols = slice(grp * GROUP * H, (grp + CHUNK) * GROUP * H)
                 nc.sync.dma_start(out=h_sb[:, cols], in_=h_rows[:, cols])
                 nc.sync.dma_start(out=c_sb[:, cols], in_=c_rows[:, cols])
 
-        def transpose(grp):
-            first = grp * GROUP
+        def transpose_state(grp):
+            hc_ps = psum_hc.tile([P, 2 * GROUP, P], BF16)
+            for t in range(GROUP):
+                cols = slice((grp * GROUP + t) * H, (grp * GROUP + t + 1) * H)
+                nc.tensor.transpose(hc_ps[:, t, :], h_sb[:, cols], ident_bf[:])
+                nc.tensor.transpose(hc_ps[:, GROUP + t, :], c_sb[:, cols], ident_bf[:])
+            hc_t = x_pool.tile([P, 2 * GROUP, P], BF16)
+            nc.scalar.copy(out=hc_t[:], in_=hc_ps[:])
+            hc_side[grp] = hc_t
+
+        def transpose_x(grp):
             x_words = x_in[grp][:].rearrange("p n k -> p (n k)").bitcast(F32)
             x_grouped = two.tile([P, GROUP * K], BF16, align_bytes=64)
             grouped_words = x_grouped[:].bitcast(F32)
@@ -142,14 +173,6 @@ def tile_multiinputlstmcell_pa_t_kernel(
                     in_=x_t[:].rearrange("p (g u) r -> p g r u", u=2),
                 )
             x_side[grp] = x_grouped
-            hc_ps = psum_hc.tile([P, 2 * GROUP, P], BF16)
-            for t in range(GROUP):
-                cols = slice((first + t) * H, (first + t + 1) * H)
-                nc.tensor.transpose(hc_ps[:, t, :], h_sb[:, cols], ident_bf[:])
-                nc.tensor.transpose(hc_ps[:, GROUP + t, :], c_sb[:, cols], ident_bf[:])
-            hc_t = two.tile([P, 2 * GROUP, P], BF16)
-            nc.scalar.copy(out=hc_t[:], in_=hc_ps[:])
-            hc_side[grp] = hc_t
 
         def quantise(grp):
             x_codes = two.tile([P, GROUP * PASSES * P], U32, align_bytes=64)
@@ -160,21 +183,19 @@ def tile_multiinputlstmcell_pa_t_kernel(
             x_code[grp] = x_codes
             x_scale[grp] = x_scales
 
-        def plain_product(grp, t, pre):
-            hc_t = hc_side[grp]
+        def plain_product(grp, t):
+            if t == 0:
+                pre = pre_pool.tile([P, GROUP, GATES], F32)
+                pre_of[grp] = pre
+            h_t = hc_side[grp][:, t, :]
+            c_t = hc_side[grp][:, GROUP + t, :]
             plain = psum_plain.tile([P, GATES], F32)
-            nc.tensor.matmul(
-                plain[:, 0 : 2 * H], lhsT=hc_t[:, t, :], rhs=whh[:, 0 : 2 * H], start=True, stop=True
-            )
-            nc.tensor.matmul(
-                plain[:, 2 * H : SIG], lhsT=hc_t[:, GROUP + t, :], rhs=awhh[:], start=True, stop=True
-            )
-            nc.tensor.matmul(
-                plain[:, SIG:GATES], lhsT=hc_t[:, t, :], rhs=whh[:, 2 * H : SIG], start=True, stop=True
-            )
-            nc.vector.tensor_tensor(out=pre[:, t, :], in0=plain[:], in1=bias_all[:], op=ALU.add)
+            nc.tensor.matmul(plain[:, 0 : 2 * H], lhsT=h_t, rhs=whh[:, 0 : 2 * H], start=True, stop=True)
+            nc.tensor.matmul(plain[:, 2 * H : SIG], lhsT=c_t, rhs=awhh[:], start=True, stop=True)
+            nc.tensor.matmul(plain[:, SIG:GATES], lhsT=h_t, rhs=whh[:, 2 * H : SIG], start=True, stop=True)
+            nc.vector.tensor_tensor(out=pre_of[grp][:, t, :], in0=plain[:], in1=bias_all[:], op=ALU.add)
 
-        def mx_product(grp, t, pre):
+        def mx_product(grp, t):
             acc = psum_mx.tile([P, GATES], F32)
             for g in range(PASSES):
                 lo = (t * PASSES + g) * P
@@ -187,20 +208,12 @@ def tile_multiinputlstmcell_pa_t_kernel(
                     start=(g == 0),
                     stop=(g == PASSES - 1),
                 )
-            nc.vector.tensor_tensor(out=pre[:, t, :], in0=acc[:], in1=pre[:, t, :], op=ALU.add)
-
-        def products(grp):
-            pre = two.tile([P, GROUP, GATES], F32)
-            for t in range(GROUP + 1):
-                if t < GROUP:
-                    plain_product(grp, t, pre)
-                if t > 0:
-                    mx_product(grp, t - 1, pre)
-            pre_of[grp] = pre
+            pre_t = pre_of[grp][:, t, :]
+            nc.vector.tensor_tensor(out=pre_t, in0=acc[:], in1=pre_t, op=ALU.add)
 
         def activate(grp):
             pre = pre_of[grp]
-            gates = four.tile([P, GROUP, GATES], F32)
+            gates = gates_pool.tile([P, GROUP, GATES], F32)
             nc.scalar.activation(out=gates[:, :, 0:SIG], in_=pre[:, :, 0:SIG], func=ACT.Sigmoid)
             nc.scalar.activation(out=gates[:, :, SIG:GATES], in_=pre[:, :, SIG:GATES], func=ACT.Tanh)
             gates_of[grp] = gates
@@ -218,23 +231,22 @@ def tile_multiinputlstmcell_pa_t_kernel(
             nc.scalar.activation(out=w_i[:], in_=diff_of[grp][:], func=ACT.Sigmoid)
             w_of[grp] = w_i
 
-        def g_minus_c(grp):
+        def g_minus_c(grp, engine):
             move = two.tile([P, GROUP, H], F32)
-            nc.gpsimd.tensor_tensor(
+            engine.tensor_tensor(
                 out=move[:], in0=gates_of[grp][:, :, SIG:GATES], in1=c_in_of(grp), op=ALU.subtract
             )
             move_of[grp] = move
 
-        def weighted_move(grp):
+        def weighted_move(grp, engine):
             step = two.tile([P, GROUP, H], F32)
-            nc.gpsimd.tensor_tensor(out=step[:], in0=w_of[grp][:], in1=move_of[grp][:], op=ALU.mult)
+            engine.tensor_tensor(out=step[:], in0=w_of[grp][:], in1=move_of[grp][:], op=ALU.mult)
             step_of[grp] = step
 
-        def new_cell(grp):
-            first = grp * GROUP
+        def new_cell(grp, engine):
             c_1 = two.tile([P, GROUP, H], F32)
-            nc.gpsimd.tensor_tensor(out=c_1[:], in0=step_of[grp][:], in1=c_in_of(grp), op=ALU.add)
-            nc.sync.dma_start(out=c1_rows[:, first : first + GROUP, :], in_=c_1[:])
+            engine.tensor_tensor(out=c_1[:], in0=step_of[grp][:], in1=c_in_of(grp), op=ALU.add)
+            nc.sync.dma_start(out=c1_rows[:, rows_of(grp), :], in_=c_1[:])
             c1_of[grp] = c_1
 
         def tanh_cell(grp):
@@ -242,29 +254,38 @@ def tile_multiinputlstmcell_pa_t_kernel(
             nc.scalar.activation(out=tanh_c[:], in_=c1_of[grp][:], func=ACT.Tanh)
             tanh_of[grp] = tanh_c
 
-        def new_hidden(grp):
-            first = grp * GROUP
+        def new_hidden(grp, engine):
             h_1 = two.tile([P, GROUP, H], F32)
-            nc.gpsimd.tensor_tensor(
+            engine.tensor_tensor(
                 out=h_1[:], in0=gates_of[grp][:, :, H : 2 * H], in1=tanh_of[grp][:], op=ALU.mult
             )
-            nc.sync.dma_start(out=h1_rows[:, first : first + GROUP, :], in_=h_1[:])
+            nc.sync.dma_start(out=h1_rows[:, rows_of(grp), :], in_=h_1[:])
 
-        def run(stage, grp):
+        def run(stage, grp, *more):
             if 0 <= grp < N_GROUPS:
-                stage(grp)
+                stage(grp, *more)
 
         with tc.manual_schedule():
-            for rnd in range(-3, N_GROUPS + 4):
-                run(load, rnd + 3)
+            for rnd in range(-LEAD - 3, N_GROUPS + 4):
+                tail = nc.gpsimd if rnd + LEAD < N_GROUPS else nc.vector
+                run(load_x, rnd + 3)
+                run(load_state, rnd + LEAD + 3)
+                if rnd + LEAD + 3 == 0:
+                    load_weights()
                 run(activate, rnd - 1)
                 run(pair_weight, rnd - 2)
-                run(weighted_move, rnd - 3)
-                run(g_minus_c, rnd - 2)
-                run(new_cell, rnd - 3)
-                run(new_hidden, rnd - 4)
-                run(products, rnd)
-                run(transpose, rnd + 2)
+                for t in range(GROUP):
+                    run(plain_product, rnd + LEAD, t)
+                    run(mx_product, rnd, t)
+                run(transpose_x, rnd + 2)
+                run(transpose_state, rnd + LEAD + 2)
+                if rnd + 1 == 0:
+                    regroup_weights()
+                    quantise_weights()
                 run(quantise, rnd + 1)
+                run(weighted_move, rnd - 3, tail)
+                run(g_minus_c, rnd - 2, tail)
+                run(new_cell, rnd - 3, tail)
+                run(new_hidden, rnd - 4, tail)
                 run(gate_difference, rnd - 1)
                 run(tanh_cell, rnd - 3)

@@ -24,6 +24,7 @@ GROUP = 4
 N_GROUPS = TILES // GROUP
 CHUNK = 2
 LEAD = 1
+SCALAR_TILE = GROUP - 1
 
 FLOPS = 2 * ROWS * (K + H) * GATES
 
@@ -190,10 +191,22 @@ def tile_multiinputlstmcell_pa_t_kernel(
             h_t = hc_side[grp][:, t, :]
             c_t = hc_side[grp][:, GROUP + t, :]
             plain = psum_plain.tile([P, GATES], F32)
-            nc.tensor.matmul(plain[:, 0 : 2 * H], lhsT=h_t, rhs=whh[:, 0 : 2 * H], start=True, stop=True)
-            nc.tensor.matmul(plain[:, 2 * H : SIG], lhsT=c_t, rhs=awhh[:], start=True, stop=True)
-            nc.tensor.matmul(plain[:, SIG:GATES], lhsT=h_t, rhs=whh[:, 2 * H : SIG], start=True, stop=True)
-            nc.vector.tensor_tensor(out=pre_of[grp][:, t, :], in0=plain[:], in1=bias_all[:], op=ALU.add)
+            by_scalar = t == SCALAR_TILE
+            if by_scalar:
+                nc.tensor.matmul(plain[:], lhsT=ones[:], rhs=bias_row[:], start=True, stop=False)
+            nc.tensor.matmul(
+                plain[:, 0 : 2 * H], lhsT=h_t, rhs=whh[:, 0 : 2 * H], start=not by_scalar, stop=not by_scalar
+            )
+            nc.tensor.matmul(
+                plain[:, 2 * H : SIG], lhsT=c_t, rhs=awhh[:], start=not by_scalar, stop=not by_scalar
+            )
+            nc.tensor.matmul(
+                plain[:, SIG:GATES], lhsT=h_t, rhs=whh[:, 2 * H : SIG], start=not by_scalar, stop=True
+            )
+            if by_scalar:
+                nc.scalar.copy(out=pre_of[grp][:, t, :], in_=plain[:])
+            else:
+                nc.vector.tensor_tensor(out=pre_of[grp][:, t, :], in0=plain[:], in1=bias_all[:], op=ALU.add)
 
         def mx_product(grp, t):
             acc = psum_mx.tile([P, GATES], F32)
@@ -286,6 +299,6 @@ def tile_multiinputlstmcell_pa_t_kernel(
                 run(weighted_move, rnd - 3, tail)
                 run(g_minus_c, rnd - 2, tail)
                 run(new_cell, rnd - 3, tail)
-                run(new_hidden, rnd - 4, tail)
+                run(new_hidden, rnd - 4, nc.vector)
                 run(gate_difference, rnd - 1)
                 run(tanh_cell, rnd - 3)

@@ -21,8 +21,11 @@ PASSES = K // K_PASS
 WORDS = K // 2
 TILES = ROWS // P
 GROUP = 4
-N_GROUPS = TILES // GROUP
-CHUNK = 2
+TAPER = [1, 1, 2]
+SIZES = TAPER + [GROUP] * ((TILES - 2 * sum(TAPER)) // GROUP) + TAPER[::-1]
+FIRST = [sum(SIZES[:grp]) for grp in range(len(SIZES))]
+N_GROUPS = len(SIZES)
+CHUNK = 2 * GROUP
 LEAD = 1
 SCALAR_TILE = GROUP - 1
 
@@ -71,9 +74,8 @@ def tile_multiinputlstmcell_pa_t_kernel(
 
         bias_row = consts.tile([P, GATES], BF16)
         nc.vector.memset(bias_row[:], 0.0)
-        nc.scalar.dma_start(out=bias_row[0:1, 0 : 2 * H], in_=bias[0 : 2 * H].unsqueeze(0))
-        nc.scalar.dma_start(out=bias_row[0:1, 2 * H : SIG], in_=alpha_bias.unsqueeze(0))
-        nc.scalar.dma_start(out=bias_row[0:1, SIG:GATES], in_=bias[2 * H : SIG].unsqueeze(0))
+        nc.scalar.dma_start(out=bias_row[0:1, H:GATES], in_=bias.unsqueeze(0))
+        nc.scalar.dma_start(out=bias_row[0:1, 0:H], in_=alpha_bias.unsqueeze(0))
         ones = consts.tile([P, P], BF16)
         nc.vector.memset(ones[:], 1.0)
         bias_ps = psum_plain.tile([P, GATES], F32, tag="plain")
@@ -95,27 +97,25 @@ def tile_multiinputlstmcell_pa_t_kernel(
         c_sb = consts.tile([P, TILES * H], BF16)
 
         def load_weights():
-            nc.sync.dma_start(
-                out=w_raw[:].rearrange("p g (u e) c -> p (g u) (e c)", e=2),
-                in_=weight_ih.rearrange("(j p e) c -> p j (e c)", p=P, e=2),
-            )
-            nc.sync.dma_start(
-                out=a_raw[:].rearrange("p g (u e) c -> p (g u) (e c)", e=2),
-                in_=alpha_weight_ih.rearrange("(j p e) c -> p j (e c)", p=P, e=2),
-            )
+            for g in range(PASSES):
+                k_rows = slice(g * K_PASS, (g + 1) * K_PASS)
+                nc.sync.dma_start(
+                    out=w_raw[:, g, :, :].rearrange("p (u e) c -> p u (e c)", e=2),
+                    in_=weight_ih[k_rows, :].rearrange("(u p e) c -> p u (e c)", p=P, e=2),
+                )
+                nc.sync.dma_start(
+                    out=a_raw[:, g, :, :].rearrange("p (u e) c -> p u (e c)", e=2),
+                    in_=alpha_weight_ih[k_rows, :].rearrange("(u p e) c -> p u (e c)", p=P, e=2),
+                )
 
         def regroup_weights():
             for g in range(PASSES):
                 nc.vector.tensor_copy(
-                    out=w_grouped[:, g, 0 : 2 * H, :],
-                    in_=w_raw[:, g, :, 0 : 2 * H].rearrange("p t c -> p c t"),
+                    out=w_grouped[:, g, H:GATES, :],
+                    in_=w_raw[:, g, :, :].rearrange("p t c -> p c t"),
                 )
                 nc.vector.tensor_copy(
-                    out=w_grouped[:, g, SIG:GATES, :],
-                    in_=w_raw[:, g, :, 2 * H : SIG].rearrange("p t c -> p c t"),
-                )
-                nc.vector.tensor_copy(
-                    out=w_grouped[:, g, 2 * H : SIG, :],
+                    out=w_grouped[:, g, 0:H, :],
                     in_=a_raw[:, g, :, :].rearrange("p t c -> p c t"),
                 )
 
@@ -131,38 +131,42 @@ def tile_multiinputlstmcell_pa_t_kernel(
         pre_of, gates_of, diff_of, w_of, move_of, step_of, c1_of, tanh_of = {}, {}, {}, {}, {}, {}, {}, {}
 
         def rows_of(grp):
-            return slice(grp * GROUP, (grp + 1) * GROUP)
+            return slice(FIRST[grp], FIRST[grp] + SIZES[grp])
 
         def c_in_of(grp):
-            lo = grp * GROUP * H
-            return c_sb[:, lo : lo + GROUP * H].rearrange("p (n h) -> p n h", h=H)
+            lo = FIRST[grp] * H
+            return c_sb[:, lo : lo + SIZES[grp] * H].rearrange("p (n h) -> p n h", h=H)
+
 
         def load_x(grp):
             x_sb = x_pool.tile([P, GROUP, K], BF16)
-            nc.sync.dma_start(out=x_sb[:], in_=x_rows[:, rows_of(grp), :])
+            nc.sync.dma_start(out=x_sb[:, 0 : SIZES[grp], :], in_=x_rows[:, rows_of(grp), :])
             x_in[grp] = x_sb
 
         def load_state(grp):
-            if grp % CHUNK == 0:
-                cols = slice(grp * GROUP * H, (grp + CHUNK) * GROUP * H)
+            lo = FIRST[grp]
+            if lo == 0 or (lo - sum(TAPER)) % CHUNK == 0:
+                hi = min(lo + CHUNK, TILES) if lo else sum(TAPER)
+                cols = slice(lo * H, hi * H)
                 nc.sync.dma_start(out=h_sb[:, cols], in_=h_rows[:, cols])
                 nc.sync.dma_start(out=c_sb[:, cols], in_=c_rows[:, cols])
 
         def transpose_state(grp):
             hc_ps = psum_hc.tile([P, 2 * GROUP, P], BF16)
-            for t in range(GROUP):
-                cols = slice((grp * GROUP + t) * H, (grp * GROUP + t + 1) * H)
+            n = SIZES[grp]
+            for t in range(n):
+                cols = slice((FIRST[grp] + t) * H, (FIRST[grp] + t + 1) * H)
                 nc.tensor.transpose(hc_ps[:, t, :], h_sb[:, cols], ident_bf[:])
-                nc.tensor.transpose(hc_ps[:, GROUP + t, :], c_sb[:, cols], ident_bf[:])
+                nc.tensor.transpose(hc_ps[:, n + t, :], c_sb[:, cols], ident_bf[:])
             hc_t = x_pool.tile([P, 2 * GROUP, P], BF16)
-            nc.scalar.copy(out=hc_t[:], in_=hc_ps[:])
+            nc.scalar.copy(out=hc_t[:, 0 : 2 * n, :], in_=hc_ps[:, 0 : 2 * n, :])
             hc_side[grp] = hc_t
 
         def transpose_x(grp):
             x_words = x_in[grp][:].rearrange("p n k -> p (n k)").bitcast(F32)
             x_grouped = two.tile([P, GROUP * K], BF16, align_bytes=64)
             grouped_words = x_grouped[:].bitcast(F32)
-            for t in range(GROUP):
+            for t in range(SIZES[grp]):
                 x_t = psum_x.tile([P, 2 * PASSES, P], F32)
                 for j in range(2 * PASSES):
                     lo = t * WORDS + j * P
@@ -178,8 +182,11 @@ def tile_multiinputlstmcell_pa_t_kernel(
         def quantise(grp):
             x_codes = two.tile([P, GROUP * PASSES * P], U32, align_bytes=64)
             x_scales = two.tile([P, GROUP * PASSES * P], U8, align_bytes=64)
+            words = SIZES[grp] * PASSES * P
             nc.vector.quantize_mx(
-                out=x_codes[:].bitcast(FP8X4), scales=x_scales[:], in_=x_side[grp][:]
+                out=x_codes[:, 0:words].bitcast(FP8X4),
+                scales=x_scales[:, 0:words],
+                in_=x_side[grp][:, 0 : PACK * words],
             )
             x_code[grp] = x_codes
             x_scale[grp] = x_scales
@@ -189,20 +196,15 @@ def tile_multiinputlstmcell_pa_t_kernel(
                 pre = pre_pool.tile([P, GROUP, GATES], F32)
                 pre_of[grp] = pre
             h_t = hc_side[grp][:, t, :]
-            c_t = hc_side[grp][:, GROUP + t, :]
+            c_t = hc_side[grp][:, SIZES[grp] + t, :]
             plain = psum_plain.tile([P, GATES], F32)
             by_scalar = t == SCALAR_TILE
             if by_scalar:
                 nc.tensor.matmul(plain[:], lhsT=ones[:], rhs=bias_row[:], start=True, stop=False)
             nc.tensor.matmul(
-                plain[:, 0 : 2 * H], lhsT=h_t, rhs=whh[:, 0 : 2 * H], start=not by_scalar, stop=not by_scalar
+                plain[:, H:GATES], lhsT=h_t, rhs=whh[:], start=not by_scalar, stop=not by_scalar
             )
-            nc.tensor.matmul(
-                plain[:, 2 * H : SIG], lhsT=c_t, rhs=awhh[:], start=not by_scalar, stop=not by_scalar
-            )
-            nc.tensor.matmul(
-                plain[:, SIG:GATES], lhsT=h_t, rhs=whh[:, 2 * H : SIG], start=not by_scalar, stop=True
-            )
+            nc.tensor.matmul(plain[:, 0:H], lhsT=c_t, rhs=awhh[:], start=not by_scalar, stop=True)
             if by_scalar:
                 nc.scalar.copy(out=pre_of[grp][:, t, :], in_=plain[:])
             else:
@@ -225,80 +227,85 @@ def tile_multiinputlstmcell_pa_t_kernel(
             nc.vector.tensor_tensor(out=pre_t, in0=acc[:], in1=pre_t, op=ALU.add)
 
         def activate(grp):
-            pre = pre_of[grp]
             gates = gates_pool.tile([P, GROUP, GATES], F32)
-            nc.scalar.activation(out=gates[:, :, 0:SIG], in_=pre[:, :, 0:SIG], func=ACT.Sigmoid)
-            nc.scalar.activation(out=gates[:, :, SIG:GATES], in_=pre[:, :, SIG:GATES], func=ACT.Tanh)
-            gates_of[grp] = gates
+            gates_of[grp] = gates[:, 0 : SIZES[grp], :]
+            pre = pre_of[grp][:, 0 : SIZES[grp], :]
+            nc.scalar.activation(out=gates_of[grp][:, :, 0:SIG], in_=pre[:, :, 0:SIG], func=ACT.Sigmoid)
+            nc.scalar.activation(out=gates_of[grp][:, :, SIG:GATES], in_=pre[:, :, SIG:GATES], func=ACT.Tanh)
 
         def gate_difference(grp):
             gates = gates_of[grp]
             diff = two.tile([P, GROUP, H], F32)
+            diff_of[grp] = diff[:, 0 : SIZES[grp], :]
             nc.vector.tensor_tensor(
-                out=diff[:], in0=gates[:, :, 0:H], in1=gates[:, :, 2 * H : SIG], op=ALU.subtract
+                out=diff_of[grp], in0=gates[:, :, H : 2 * H], in1=gates[:, :, 0:H], op=ALU.subtract
             )
-            diff_of[grp] = diff
 
         def pair_weight(grp):
             w_i = two.tile([P, GROUP, H], F32)
-            nc.scalar.activation(out=w_i[:], in_=diff_of[grp][:], func=ACT.Sigmoid)
-            w_of[grp] = w_i
+            w_of[grp] = w_i[:, 0 : SIZES[grp], :]
+            nc.scalar.activation(out=w_of[grp], in_=diff_of[grp], func=ACT.Sigmoid)
 
         def g_minus_c(grp, engine):
             move = two.tile([P, GROUP, H], F32)
+            move_of[grp] = move[:, 0 : SIZES[grp], :]
             engine.tensor_tensor(
-                out=move[:], in0=gates_of[grp][:, :, SIG:GATES], in1=c_in_of(grp), op=ALU.subtract
+                out=move_of[grp], in0=gates_of[grp][:, :, SIG:GATES], in1=c_in_of(grp), op=ALU.subtract
             )
-            move_of[grp] = move
 
         def weighted_move(grp, engine):
             step = two.tile([P, GROUP, H], F32)
-            engine.tensor_tensor(out=step[:], in0=w_of[grp][:], in1=move_of[grp][:], op=ALU.mult)
-            step_of[grp] = step
+            step_of[grp] = step[:, 0 : SIZES[grp], :]
+            engine.tensor_tensor(out=step_of[grp], in0=w_of[grp], in1=move_of[grp], op=ALU.mult)
 
         def new_cell(grp, engine):
             c_1 = two.tile([P, GROUP, H], F32)
-            engine.tensor_tensor(out=c_1[:], in0=step_of[grp][:], in1=c_in_of(grp), op=ALU.add)
-            nc.sync.dma_start(out=c1_rows[:, rows_of(grp), :], in_=c_1[:])
-            c1_of[grp] = c_1
+            c1_of[grp] = c_1[:, 0 : SIZES[grp], :]
+            engine.tensor_tensor(out=c1_of[grp], in0=step_of[grp], in1=c_in_of(grp), op=ALU.add)
+            nc.sync.dma_start(out=c1_rows[:, rows_of(grp), :], in_=c1_of[grp])
 
         def tanh_cell(grp):
             tanh_c = two.tile([P, GROUP, H], F32)
-            nc.scalar.activation(out=tanh_c[:], in_=c1_of[grp][:], func=ACT.Tanh)
-            tanh_of[grp] = tanh_c
+            tanh_of[grp] = tanh_c[:, 0 : SIZES[grp], :]
+            nc.scalar.activation(out=tanh_of[grp], in_=c1_of[grp], func=ACT.Tanh)
 
         def new_hidden(grp, engine):
             h_1 = two.tile([P, GROUP, H], F32)
+            h_1 = h_1[:, 0 : SIZES[grp], :]
             engine.tensor_tensor(
-                out=h_1[:], in0=gates_of[grp][:, :, H : 2 * H], in1=tanh_of[grp][:], op=ALU.mult
+                out=h_1, in0=gates_of[grp][:, :, 2 * H : SIG], in1=tanh_of[grp], op=ALU.mult
             )
-            nc.sync.dma_start(out=h1_rows[:, rows_of(grp), :], in_=h_1[:])
+            nc.sync.dma_start(out=h1_rows[:, rows_of(grp), :], in_=h_1)
 
         def run(stage, grp, *more):
             if 0 <= grp < N_GROUPS:
                 stage(grp, *more)
 
+        def run_tile(stage, grp, t):
+            if 0 <= grp < N_GROUPS and t < SIZES[grp]:
+                stage(grp, t)
+
         with tc.manual_schedule():
-            for rnd in range(-LEAD - 3, N_GROUPS + 4):
+            for rnd in range(-LEAD - 3, N_GROUPS + 3):
                 tail = nc.gpsimd if rnd + LEAD < N_GROUPS else nc.vector
-                run(load_x, rnd + 3)
-                run(load_state, rnd + LEAD + 3)
                 if rnd + LEAD + 3 == 0:
                     load_weights()
+                run(load_x, rnd + 3)
+                run(load_state, rnd + LEAD + 3)
                 run(activate, rnd - 1)
-                run(pair_weight, rnd - 2)
                 for t in range(GROUP):
-                    run(plain_product, rnd + LEAD, t)
-                    run(mx_product, rnd, t)
+                    run_tile(plain_product, rnd + LEAD, t)
+                    run_tile(mx_product, rnd, t)
+                run(weighted_move, rnd - 2, tail)
+                run(new_cell, rnd - 2, tail)
+                run(g_minus_c, rnd - 1, tail)
                 run(transpose_x, rnd + 2)
+                run(tanh_cell, rnd - 2)
                 run(transpose_state, rnd + LEAD + 2)
-                if rnd + 1 == 0:
+                if rnd + LEAD + 2 == 0:
                     regroup_weights()
                     quantise_weights()
                 run(quantise, rnd + 1)
-                run(weighted_move, rnd - 3, tail)
-                run(g_minus_c, rnd - 2, tail)
-                run(new_cell, rnd - 3, tail)
-                run(new_hidden, rnd - 4, nc.vector)
                 run(gate_difference, rnd - 1)
-                run(tanh_cell, rnd - 3)
+                run(pair_weight, rnd - 1)
+                run(new_hidden, rnd - 3, nc.vector)

@@ -78,10 +78,7 @@ def tile_multiinputlstmcell_pa_t_kernel(
         nc.scalar.dma_start(out=bias_row[0:1, 0:H], in_=alpha_bias.unsqueeze(0))
         ones = consts.tile([P, P], BF16)
         nc.vector.memset(ones[:], 1.0)
-        bias_ps = psum_plain.tile([P, GATES], F32, tag="plain")
-        nc.tensor.matmul(bias_ps[:], lhsT=ones[:], rhs=bias_row[:], start=True, stop=True)
         bias_all = consts.tile([P, GATES], F32)
-        nc.vector.tensor_copy(out=bias_all[:], in_=bias_ps[:])
 
         ident_f32 = consts.tile([P, P], F32)
         make_identity(nc, ident_f32[:])
@@ -126,6 +123,11 @@ def tile_multiinputlstmcell_pa_t_kernel(
                     scales=w_scales[:, g, :],
                     in_=w_grouped[:, g, :, :].rearrange("p c t -> p (c t)"),
                 )
+
+        def spread_bias():
+            bias_ps = psum_plain.tile([P, GATES], F32, tag="plain")
+            nc.tensor.matmul(bias_ps[:], lhsT=ones[:], rhs=bias_row[:], start=True, stop=True)
+            nc.vector.tensor_copy(out=bias_all[:], in_=bias_ps[:])
 
         x_in, x_side, x_code, x_scale, hc_side = {}, {}, {}, {}, {}
         pre_of, gates_of, diff_of, w_of, move_of, step_of, c1_of, tanh_of = {}, {}, {}, {}, {}, {}, {}, {}
@@ -198,7 +200,7 @@ def tile_multiinputlstmcell_pa_t_kernel(
             h_t = hc_side[grp][:, t, :]
             c_t = hc_side[grp][:, SIZES[grp] + t, :]
             plain = psum_plain.tile([P, GATES], F32)
-            by_scalar = t == SCALAR_TILE
+            by_scalar = t == SCALAR_TILE and grp % 2 == 0
             if by_scalar:
                 nc.tensor.matmul(plain[:], lhsT=ones[:], rhs=bias_row[:], start=True, stop=False)
             nc.tensor.matmul(
@@ -230,8 +232,8 @@ def tile_multiinputlstmcell_pa_t_kernel(
             gates = gates_pool.tile([P, GROUP, GATES], F32)
             gates_of[grp] = gates[:, 0 : SIZES[grp], :]
             pre = pre_of[grp][:, 0 : SIZES[grp], :]
-            nc.scalar.activation(out=gates_of[grp][:, :, 0:SIG], in_=pre[:, :, 0:SIG], func=ACT.Sigmoid)
             nc.scalar.activation(out=gates_of[grp][:, :, SIG:GATES], in_=pre[:, :, SIG:GATES], func=ACT.Tanh)
+            nc.scalar.activation(out=gates_of[grp][:, :, 0:SIG], in_=pre[:, :, 0:SIG], func=ACT.Sigmoid)
 
         def gate_difference(grp):
             gates = gates_of[grp]
@@ -259,7 +261,7 @@ def tile_multiinputlstmcell_pa_t_kernel(
             engine.tensor_tensor(out=step_of[grp], in0=w_of[grp], in1=move_of[grp], op=ALU.mult)
 
         def new_cell(grp, engine):
-            c_1 = two.tile([P, GROUP, H], F32)
+            c_1 = gates_pool.tile([P, GROUP, H], F32)
             c1_of[grp] = c_1[:, 0 : SIZES[grp], :]
             engine.tensor_tensor(out=c1_of[grp], in0=step_of[grp], in1=c_in_of(grp), op=ALU.add)
             nc.sync.dma_start(out=c1_rows[:, rows_of(grp), :], in_=c1_of[grp])
@@ -270,7 +272,7 @@ def tile_multiinputlstmcell_pa_t_kernel(
             nc.scalar.activation(out=tanh_of[grp], in_=c1_of[grp], func=ACT.Tanh)
 
         def new_hidden(grp, engine):
-            h_1 = two.tile([P, GROUP, H], F32)
+            h_1 = gates_pool.tile([P, GROUP, H], F32)
             h_1 = h_1[:, 0 : SIZES[grp], :]
             engine.tensor_tensor(
                 out=h_1, in0=gates_of[grp][:, :, 2 * H : SIG], in1=tanh_of[grp], op=ALU.mult
@@ -287,7 +289,7 @@ def tile_multiinputlstmcell_pa_t_kernel(
 
         with tc.manual_schedule():
             for rnd in range(-LEAD - 3, N_GROUPS + 3):
-                tail = nc.gpsimd if rnd + LEAD < N_GROUPS else nc.vector
+                tail = nc.gpsimd if rnd + 2 < N_GROUPS else nc.vector
                 if rnd + LEAD + 3 == 0:
                     load_weights()
                 run(load_x, rnd + 3)
@@ -296,16 +298,17 @@ def tile_multiinputlstmcell_pa_t_kernel(
                 for t in range(GROUP):
                     run_tile(plain_product, rnd + LEAD, t)
                     run_tile(mx_product, rnd, t)
-                run(weighted_move, rnd - 2, tail)
-                run(new_cell, rnd - 2, tail)
-                run(g_minus_c, rnd - 1, tail)
                 run(transpose_x, rnd + 2)
-                run(tanh_cell, rnd - 2)
-                run(transpose_state, rnd + LEAD + 2)
                 if rnd + LEAD + 2 == 0:
                     regroup_weights()
                     quantise_weights()
+                    spread_bias()
                 run(quantise, rnd + 1)
+                run(weighted_move, rnd - 2, tail)
+                run(new_cell, rnd - 2, tail)
+                run(g_minus_c, rnd - 1, tail)
+                run(tanh_cell, rnd - 2)
                 run(gate_difference, rnd - 1)
                 run(pair_weight, rnd - 1)
+                run(transpose_state, rnd + LEAD + 2)
                 run(new_hidden, rnd - 3, nc.vector)

@@ -200,7 +200,7 @@ def tile_multiinputlstmcell_pa_t_kernel(
             h_t = hc_side[grp][:, t, :]
             c_t = hc_side[grp][:, SIZES[grp] + t, :]
             plain = psum_plain.tile([P, GATES], F32)
-            by_scalar = t == SCALAR_TILE and grp % 2 == 0
+            by_scalar = t == SCALAR_TILE
             if by_scalar:
                 nc.tensor.matmul(plain[:], lhsT=ones[:], rhs=bias_row[:], start=True, stop=False)
             nc.tensor.matmul(

@@ -288,7 +288,7 @@ def tile_multiinputlstmcell_pa_t_kernel(
                 stage(grp, t)
 
         with tc.manual_schedule():
-            for rnd in range(-LEAD - 3, N_GROUPS + 3):
+            for rnd in range(-LEAD - 3, N_GROUPS + 2):
                 tail = nc.gpsimd if rnd + 2 < N_GROUPS else nc.vector
                 if rnd + LEAD + 3 == 0:
                     load_weights()
@@ -303,12 +303,12 @@ def tile_multiinputlstmcell_pa_t_kernel(
                     regroup_weights()
                     quantise_weights()
                     spread_bias()
-                run(quantise, rnd + 1)
-                run(weighted_move, rnd - 2, tail)
-                run(new_cell, rnd - 2, tail)
-                run(g_minus_c, rnd - 1, tail)
-                run(tanh_cell, rnd - 2)
                 run(gate_difference, rnd - 1)
+                run(quantise, rnd + 1)
+                run(g_minus_c, rnd - 1, nc.vector)
                 run(pair_weight, rnd - 1)
                 run(transpose_state, rnd + LEAD + 2)
-                run(new_hidden, rnd - 3, nc.vector)
+                run(weighted_move, rnd - 1, tail)
+                run(new_cell, rnd - 1, tail)
+                run(tanh_cell, rnd - 2)
+                run(new_hidden, rnd - 2, tail)

@@ -200,7 +200,7 @@ def tile_multiinputlstmcell_pa_t_kernel(
             h_t = hc_side[grp][:, t, :]
             c_t = hc_side[grp][:, SIZES[grp] + t, :]
             plain = psum_plain.tile([P, GATES], F32)
-            by_scalar = t == SCALAR_TILE
+            by_scalar = t == SCALAR_TILE and grp % 2 == 0
             if by_scalar:
                 nc.tensor.matmul(plain[:], lhsT=ones[:], rhs=bias_row[:], start=True, stop=False)
             nc.tensor.matmul(

@@ -25,7 +25,6 @@ TAPER = [1, 1, 2]
 SIZES = TAPER + [GROUP] * ((TILES - 2 * sum(TAPER)) // GROUP) + TAPER[::-1]
 FIRST = [sum(SIZES[:grp]) for grp in range(len(SIZES))]
 N_GROUPS = len(SIZES)
-CHUNK = 2 * GROUP
 LEAD = 1
 SCALAR_TILE = GROUP - 1
 
@@ -48,11 +47,7 @@ def tile_multiinputlstmcell_pa_t_kernel(
 ):
     nc = tc.nc
 
-    x_rows = input_.rearrange("(p n) k -> p n k", n=TILES)
-    h_rows = h_0.rearrange("(p n) h -> p (n h)", n=TILES)
-    c_rows = c_input.rearrange("(p n) o h -> p (n o h)", n=TILES)
-    h1_rows = out_0.rearrange("(p n) h -> p n h", n=TILES)
-    c1_rows = out_1.rearrange("(p n) h -> p n h", n=TILES)
+    c_rows = c_input.rearrange("r o h -> r (o h)")
 
     with tc.tile_pool(name="consts", bufs=1) as consts, tc.tile_pool(
         name="two", bufs=2
@@ -132,8 +127,9 @@ def tile_multiinputlstmcell_pa_t_kernel(
         x_in, x_side, x_code, x_scale, hc_side = {}, {}, {}, {}, {}
         pre_of, gates_of, diff_of, w_of, move_of, step_of, c1_of, tanh_of = {}, {}, {}, {}, {}, {}, {}, {}
 
-        def rows_of(grp):
-            return slice(FIRST[grp], FIRST[grp] + SIZES[grp])
+        def rows_of(dram, grp):
+            block = dram[FIRST[grp] * P : (FIRST[grp] + SIZES[grp]) * P, :]
+            return block.rearrange("(p n) w -> p n w", n=SIZES[grp])
 
         def c_in_of(grp):
             lo = FIRST[grp] * H
@@ -142,16 +138,22 @@ def tile_multiinputlstmcell_pa_t_kernel(
 
         def load_x(grp):
             x_sb = x_pool.tile([P, GROUP, K], BF16)
-            nc.sync.dma_start(out=x_sb[:, 0 : SIZES[grp], :], in_=x_rows[:, rows_of(grp), :])
+            nc.sync.dma_start(out=x_sb[:, 0 : SIZES[grp], :], in_=rows_of(input_, grp))
             x_in[grp] = x_sb
 
         def load_state(grp):
-            lo = FIRST[grp]
-            if lo == 0 or (lo - sum(TAPER)) % CHUNK == 0:
-                hi = min(lo + CHUNK, TILES) if lo else sum(TAPER)
-                cols = slice(lo * H, hi * H)
-                nc.sync.dma_start(out=h_sb[:, cols], in_=h_rows[:, cols])
-                nc.sync.dma_start(out=c_sb[:, cols], in_=c_rows[:, cols])
+            n = SIZES[grp]
+            whole = grp - len(TAPER)
+            if n == GROUP and whole % 2 == 1:
+                return
+            last = grp + 1 if n == GROUP else grp
+            tiles = slice(FIRST[grp], FIRST[last] + n)
+            cols = slice(tiles.start * H, tiles.stop * H)
+            for sb, dram in ((h_sb, h_0), (c_sb, c_rows)):
+                nc.sync.dma_start(
+                    out=sb[:, cols].rearrange("p (g w) -> p g w", w=n * H),
+                    in_=dram[tiles.start * P : tiles.stop * P, :].rearrange("(g p n) h -> p g (n h)", p=P, n=n),
+                )
 
         def transpose_state(grp):
             hc_ps = psum_hc.tile([P, 2 * GROUP, P], BF16)
@@ -264,7 +266,7 @@ def tile_multiinputlstmcell_pa_t_kernel(
             c_1 = gates_pool.tile([P, GROUP, H], F32)
             c1_of[grp] = c_1[:, 0 : SIZES[grp], :]
             engine.tensor_tensor(out=c1_of[grp], in0=step_of[grp], in1=c_in_of(grp), op=ALU.add)
-            nc.sync.dma_start(out=c1_rows[:, rows_of(grp), :], in_=c1_of[grp])
+            nc.sync.dma_start(out=rows_of(out_1, grp), in_=c1_of[grp])
 
         def tanh_cell(grp):
             tanh_c = two.tile([P, GROUP, H], F32)
@@ -277,7 +279,7 @@ def tile_multiinputlstmcell_pa_t_kernel(
             engine.tensor_tensor(
                 out=h_1, in0=gates_of[grp][:, :, 2 * H : SIG], in1=tanh_of[grp], op=ALU.mult
             )
-            nc.sync.dma_start(out=h1_rows[:, rows_of(grp), :], in_=h_1)
+            nc.sync.dma_start(out=rows_of(out_0, grp), in_=h_1)
 
         def run(stage, grp, *more):
             if 0 <= grp < N_GROUPS:

@@ -21,8 +21,9 @@ PASSES = K // K_PASS
 WORDS = K // 2
 TILES = ROWS // P
 GROUP = 4
-TAPER = [1, 1, 2]
-SIZES = TAPER + [GROUP] * ((TILES - 2 * sum(TAPER)) // GROUP) + TAPER[::-1]
+HEAD = [1, 1, 2]
+TAIL = [2, 2]
+SIZES = HEAD + [GROUP] * ((TILES - sum(HEAD) - sum(TAIL)) // GROUP) + TAIL
 FIRST = [sum(SIZES[:grp]) for grp in range(len(SIZES))]
 N_GROUPS = len(SIZES)
 LEAD = 1
@@ -54,8 +55,8 @@ def tile_multiinputlstmcell_pa_t_kernel(
     ) as two, tc.tile_pool(name="x_pool", bufs=3) as x_pool, tc.tile_pool(
         name="gates_pool", bufs=4
     ) as gates_pool, tc.tile_pool(name="pre_pool", bufs=LEAD + 2) as pre_pool, tc.psum_pool(
-        name="psum_x", bufs=3
-    ) as psum_x, tc.psum_pool(name="psum_hc", bufs=1) as psum_hc, tc.psum_pool(
+        name="psum_x", bufs=4
+    ) as psum_x, tc.psum_pool(
         name="psum_plain", bufs=2
     ) as psum_plain, tc.psum_pool(name="psum_mx", bufs=2) as psum_mx:
         warm = consts.tile([P, 1], F32)
@@ -128,8 +129,9 @@ def tile_multiinputlstmcell_pa_t_kernel(
         pre_of, gates_of, diff_of, w_of, move_of, step_of, c1_of, tanh_of = {}, {}, {}, {}, {}, {}, {}, {}
 
         def rows_of(dram, grp):
-            block = dram[FIRST[grp] * P : (FIRST[grp] + SIZES[grp]) * P, :]
-            return block.rearrange("(p n) w -> p n w", n=SIZES[grp])
+            block, tile = FIRST[grp] // GROUP * GROUP * P, FIRST[grp] % GROUP
+            rows = dram[block : block + GROUP * P, :].rearrange("(p n) w -> p n w", n=GROUP)
+            return rows[:, tile : tile + SIZES[grp], :]
 
         def c_in_of(grp):
             lo = FIRST[grp] * H
@@ -142,12 +144,11 @@ def tile_multiinputlstmcell_pa_t_kernel(
             x_in[grp] = x_sb
 
         def load_state(grp):
-            n = SIZES[grp]
-            whole = grp - len(TAPER)
-            if n == GROUP and whole % 2 == 1:
+            lo = FIRST[grp]
+            if lo > 0 and lo % (2 * GROUP) != GROUP:
                 return
-            last = grp + 1 if n == GROUP else grp
-            tiles = slice(FIRST[grp], FIRST[last] + n)
+            n = GROUP
+            tiles = slice(lo, min(lo + 2 * GROUP, TILES) if lo > 0 else GROUP)
             cols = slice(tiles.start * H, tiles.stop * H)
             for sb, dram in ((h_sb, h_0), (c_sb, c_rows)):
                 nc.sync.dma_start(
@@ -156,7 +157,7 @@ def tile_multiinputlstmcell_pa_t_kernel(
                 )
 
         def transpose_state(grp):
-            hc_ps = psum_hc.tile([P, 2 * GROUP, P], BF16)
+            hc_ps = psum_x.tile([P, 2 * GROUP, P], BF16, tag="turn")
             n = SIZES[grp]
             for t in range(n):
                 cols = slice((FIRST[grp] + t) * H, (FIRST[grp] + t + 1) * H)
@@ -171,7 +172,7 @@ def tile_multiinputlstmcell_pa_t_kernel(
             x_grouped = two.tile([P, GROUP * K], BF16, align_bytes=64)
             grouped_words = x_grouped[:].bitcast(F32)
             for t in range(SIZES[grp]):
-                x_t = psum_x.tile([P, 2 * PASSES, P], F32)
+                x_t = psum_x.tile([P, 2 * PASSES, P], F32, tag="turn")
                 for j in range(2 * PASSES):
                     lo = t * WORDS + j * P
                     nc.tensor.transpose(x_t[:, j, :], x_words[:, lo : lo + P], ident_f32[:])
@@ -292,19 +293,22 @@ def tile_multiinputlstmcell_pa_t_kernel(
         with tc.manual_schedule():
             for rnd in range(-LEAD - 3, N_GROUPS + 2):
                 tail = nc.gpsimd if rnd + 2 < N_GROUPS else nc.vector
-                if rnd + LEAD + 3 == 0:
+                if rnd == -LEAD - 3:
                     load_weights()
                 run(load_x, rnd + 3)
                 run(load_state, rnd + LEAD + 3)
                 run(activate, rnd - 1)
-                for t in range(GROUP):
-                    run_tile(plain_product, rnd + LEAD, t)
-                    run_tile(mx_product, rnd, t)
+                if rnd + LEAD == 0:
+                    spread_bias()
+                for pair in range(0, GROUP, 2):
+                    for t in (pair, pair + 1):
+                        run_tile(plain_product, rnd + LEAD, t)
+                    for t in (pair, pair + 1):
+                        run_tile(mx_product, rnd, t)
                 run(transpose_x, rnd + 2)
                 if rnd + LEAD + 2 == 0:
                     regroup_weights()
                     quantise_weights()
-                    spread_bias()
                 run(gate_difference, rnd - 1)
                 run(quantise, rnd + 1)
                 run(g_minus_c, rnd - 1, nc.vector)

@@ -26,6 +26,8 @@ TAIL = [2, 2]
 SIZES = HEAD + [GROUP] * ((TILES - sum(HEAD) - sum(TAIL)) // GROUP) + TAIL
 FIRST = [sum(SIZES[:grp]) for grp in range(len(SIZES))]
 N_GROUPS = len(SIZES)
+CELL_BY_VECTOR = N_GROUPS - 3
+HIDDEN_BY_VECTOR = N_GROUPS - 5
 LEAD = 1
 SCALAR_TILE = GROUP - 1
 
@@ -126,7 +128,7 @@ def tile_multiinputlstmcell_pa_t_kernel(
             nc.vector.tensor_copy(out=bias_all[:], in_=bias_ps[:])
 
         x_in, x_side, x_code, x_scale, hc_side = {}, {}, {}, {}, {}
-        pre_of, gates_of, diff_of, w_of, move_of, step_of, c1_of, tanh_of = {}, {}, {}, {}, {}, {}, {}, {}
+        pre_of, gates_of, diff_of, w_of, move_of, c1_of, tanh_of, h1_of = {}, {}, {}, {}, {}, {}, {}, {}
 
         def rows_of(dram, grp):
             block, tile = FIRST[grp] // GROUP * GROUP * P, FIRST[grp] % GROUP
@@ -203,7 +205,7 @@ def tile_multiinputlstmcell_pa_t_kernel(
             h_t = hc_side[grp][:, t, :]
             c_t = hc_side[grp][:, SIZES[grp] + t, :]
             plain = psum_plain.tile([P, GATES], F32)
-            by_scalar = t == SCALAR_TILE and grp % 2 == 0
+            by_scalar = t == SCALAR_TILE
             if by_scalar:
                 nc.tensor.matmul(plain[:], lhsT=ones[:], rhs=bias_row[:], start=True, stop=False)
             nc.tensor.matmul(
@@ -235,8 +237,8 @@ def tile_multiinputlstmcell_pa_t_kernel(
             gates = gates_pool.tile([P, GROUP, GATES], F32)
             gates_of[grp] = gates[:, 0 : SIZES[grp], :]
             pre = pre_of[grp][:, 0 : SIZES[grp], :]
-            nc.scalar.activation(out=gates_of[grp][:, :, SIG:GATES], in_=pre[:, :, SIG:GATES], func=ACT.Tanh)
             nc.scalar.activation(out=gates_of[grp][:, :, 0:SIG], in_=pre[:, :, 0:SIG], func=ACT.Sigmoid)
+            nc.scalar.activation(out=gates_of[grp][:, :, SIG:GATES], in_=pre[:, :, SIG:GATES], func=ACT.Tanh)
 
         def gate_difference(grp):
             gates = gates_of[grp]
@@ -251,22 +253,20 @@ def tile_multiinputlstmcell_pa_t_kernel(
             w_of[grp] = w_i[:, 0 : SIZES[grp], :]
             nc.scalar.activation(out=w_of[grp], in_=diff_of[grp], func=ACT.Sigmoid)
 
-        def g_minus_c(grp, engine):
+        def g_minus_c(grp):
             move = two.tile([P, GROUP, H], F32)
             move_of[grp] = move[:, 0 : SIZES[grp], :]
-            engine.tensor_tensor(
+            nc.vector.tensor_tensor(
                 out=move_of[grp], in0=gates_of[grp][:, :, SIG:GATES], in1=c_in_of(grp), op=ALU.subtract
             )
 
-        def weighted_move(grp, engine):
-            step = two.tile([P, GROUP, H], F32)
-            step_of[grp] = step[:, 0 : SIZES[grp], :]
-            engine.tensor_tensor(out=step_of[grp], in0=w_of[grp], in1=move_of[grp], op=ALU.mult)
-
         def new_cell(grp, engine):
+            step = two.tile([P, GROUP, H], F32)
+            step = step[:, 0 : SIZES[grp], :]
+            engine.tensor_tensor(out=step, in0=w_of[grp], in1=move_of[grp], op=ALU.mult)
             c_1 = gates_pool.tile([P, GROUP, H], F32)
             c1_of[grp] = c_1[:, 0 : SIZES[grp], :]
-            engine.tensor_tensor(out=c1_of[grp], in0=step_of[grp], in1=c_in_of(grp), op=ALU.add)
+            engine.tensor_tensor(out=c1_of[grp], in0=step, in1=c_in_of(grp), op=ALU.add)
             nc.sync.dma_start(out=rows_of(out_1, grp), in_=c1_of[grp])
 
         def tanh_cell(grp):
@@ -274,13 +274,21 @@ def tile_multiinputlstmcell_pa_t_kernel(
             tanh_of[grp] = tanh_c[:, 0 : SIZES[grp], :]
             nc.scalar.activation(out=tanh_of[grp], in_=c1_of[grp], func=ACT.Tanh)
 
-        def new_hidden(grp, engine):
-            h_1 = gates_pool.tile([P, GROUP, H], F32)
-            h_1 = h_1[:, 0 : SIZES[grp], :]
+        def new_hidden(grp, engine, lo, hi):
+            hi = min(hi, SIZES[grp])
+            if lo >= hi:
+                return
+            if lo == 0:
+                h_1 = gates_pool.tile([P, GROUP, H], F32)
+                h1_of[grp] = h_1
             engine.tensor_tensor(
-                out=h_1, in0=gates_of[grp][:, :, 2 * H : SIG], in1=tanh_of[grp], op=ALU.mult
+                out=h1_of[grp][:, lo:hi, :],
+                in0=gates_of[grp][:, lo:hi, 2 * H : SIG],
+                in1=tanh_of[grp][:, lo:hi, :],
+                op=ALU.mult,
             )
-            nc.sync.dma_start(out=rows_of(out_0, grp), in_=h_1)
+            if hi == SIZES[grp]:
+                nc.sync.dma_start(out=rows_of(out_0, grp), in_=h1_of[grp][:, 0:hi, :])
 
         def run(stage, grp, *more):
             if 0 <= grp < N_GROUPS:
@@ -291,8 +299,7 @@ def tile_multiinputlstmcell_pa_t_kernel(
                 stage(grp, t)
 
         with tc.manual_schedule():
-            for rnd in range(-LEAD - 3, N_GROUPS + 2):
-                tail = nc.gpsimd if rnd + 2 < N_GROUPS else nc.vector
+            for rnd in range(-LEAD - 3, N_GROUPS + 3):
                 if rnd == -LEAD - 3:
                     load_weights()
                 run(load_x, rnd + 3)
@@ -309,12 +316,19 @@ def tile_multiinputlstmcell_pa_t_kernel(
                 if rnd + LEAD + 2 == 0:
                     regroup_weights()
                     quantise_weights()
+                if rnd - 2 >= CELL_BY_VECTOR:
+                    run(new_cell, rnd - 2, nc.vector)
                 run(gate_difference, rnd - 1)
                 run(quantise, rnd + 1)
-                run(g_minus_c, rnd - 1, nc.vector)
+                run(g_minus_c, rnd - 1)
+                if rnd - 3 < HIDDEN_BY_VECTOR:
+                    run(new_hidden, rnd - 3, nc.vector, 0, GROUP // 2)
                 run(pair_weight, rnd - 1)
                 run(transpose_state, rnd + LEAD + 2)
-                run(weighted_move, rnd - 1, tail)
-                run(new_cell, rnd - 1, tail)
+                if rnd - 1 < CELL_BY_VECTOR:
+                    run(new_cell, rnd - 1, nc.gpsimd)
                 run(tanh_cell, rnd - 2)
-                run(new_hidden, rnd - 2, tail)
+                if rnd - 3 < HIDDEN_BY_VECTOR:
+                    run(new_hidden, rnd - 3, nc.gpsimd, GROUP // 2, GROUP)
+                else:
+                    run(new_hidden, rnd - 3, nc.vector, 0, GROUP)

@@ -29,6 +29,7 @@ N_GROUPS = len(SIZES)
 CELL_BY_VECTOR = N_GROUPS - 3
 HIDDEN_BY_VECTOR = N_GROUPS - 5
 LEAD = 1
+EARLY = 2
 SCALAR_TILE = GROUP - 1
 
 FLOPS = 2 * ROWS * (K + H) * GATES
@@ -57,10 +58,8 @@ def tile_multiinputlstmcell_pa_t_kernel(
     ) as two, tc.tile_pool(name="x_pool", bufs=3) as x_pool, tc.tile_pool(
         name="gates_pool", bufs=4
     ) as gates_pool, tc.tile_pool(name="pre_pool", bufs=LEAD + 2) as pre_pool, tc.psum_pool(
-        name="psum_x", bufs=4
-    ) as psum_x, tc.psum_pool(
-        name="psum_plain", bufs=2
-    ) as psum_plain, tc.psum_pool(name="psum_mx", bufs=2) as psum_mx:
+        name="psum", bufs=8
+    ) as psum:
         warm = consts.tile([P, 1], F32)
         nc.vector.memset(warm[:], 0.0)
         nc.scalar.activation(out=warm[:], in_=warm[:], func=ACT.Sigmoid)
@@ -123,7 +122,7 @@ def tile_multiinputlstmcell_pa_t_kernel(
                 )
 
         def spread_bias():
-            bias_ps = psum_plain.tile([P, GATES], F32, tag="plain")
+            bias_ps = psum.tile([P, GATES], F32, tag="bank")
             nc.tensor.matmul(bias_ps[:], lhsT=ones[:], rhs=bias_row[:], start=True, stop=True)
             nc.vector.tensor_copy(out=bias_all[:], in_=bias_ps[:])
 
@@ -159,7 +158,7 @@ def tile_multiinputlstmcell_pa_t_kernel(
                 )
 
         def transpose_state(grp):
-            hc_ps = psum_x.tile([P, 2 * GROUP, P], BF16, tag="turn")
+            hc_ps = psum.tile([P, 2 * GROUP, P], BF16, tag="bank")
             n = SIZES[grp]
             for t in range(n):
                 cols = slice((FIRST[grp] + t) * H, (FIRST[grp] + t + 1) * H)
@@ -174,7 +173,7 @@ def tile_multiinputlstmcell_pa_t_kernel(
             x_grouped = two.tile([P, GROUP * K], BF16, align_bytes=64)
             grouped_words = x_grouped[:].bitcast(F32)
             for t in range(SIZES[grp]):
-                x_t = psum_x.tile([P, 2 * PASSES, P], F32, tag="turn")
+                x_t = psum.tile([P, 2 * PASSES, P], F32, tag="bank")
                 for j in range(2 * PASSES):
                     lo = t * WORDS + j * P
                     nc.tensor.transpose(x_t[:, j, :], x_words[:, lo : lo + P], ident_f32[:])
@@ -204,8 +203,8 @@ def tile_multiinputlstmcell_pa_t_kernel(
                 pre_of[grp] = pre
             h_t = hc_side[grp][:, t, :]
             c_t = hc_side[grp][:, SIZES[grp] + t, :]
-            plain = psum_plain.tile([P, GATES], F32)
-            by_scalar = t == SCALAR_TILE
+            plain = psum.tile([P, GATES], F32, tag="bank")
+            by_scalar = grp < EARLY or t == SCALAR_TILE
             if by_scalar:
                 nc.tensor.matmul(plain[:], lhsT=ones[:], rhs=bias_row[:], start=True, stop=False)
             nc.tensor.matmul(
@@ -218,7 +217,7 @@ def tile_multiinputlstmcell_pa_t_kernel(
                 nc.vector.tensor_tensor(out=pre_of[grp][:, t, :], in0=plain[:], in1=bias_all[:], op=ALU.add)
 
         def mx_product(grp, t):
-            acc = psum_mx.tile([P, GATES], F32)
+            acc = psum.tile([P, GATES], F32, tag="bank")
             for g in range(PASSES):
                 lo = (t * PASSES + g) * P
                 nc.tensor.matmul_mx(

import concourse.mybir as mybir
from concourse.masks import make_identity

BF16 = mybir.dt.bfloat16
F32 = mybir.dt.float32
U32 = mybir.dt.uint32
U8 = mybir.dt.uint8
FP8X4 = mybir.dt.float8_e4m3fn_x4
ACT = mybir.ActivationFunctionType
ALU = mybir.AluOpType

P = 128
ROWS = 8192
K = 1024
H = 128
GATES = 4 * H
SIG = 3 * H
PACK = 4
K_PASS = P * PACK
PASSES = K // K_PASS
WORDS = K // 2
TILES = ROWS // P
GROUP = 4
HEAD = [1, 1, 2]
TAIL = [2, 2]
SIZES = HEAD + [GROUP] * ((TILES - sum(HEAD) - sum(TAIL)) // GROUP) + TAIL
FIRST = [sum(SIZES[:grp]) for grp in range(len(SIZES))]
N_GROUPS = len(SIZES)
CELL_BY_VECTOR = N_GROUPS - 3
HIDDEN_BY_VECTOR = N_GROUPS - 5
LEAD = 1
EARLY = 2
SCALAR_TILE = GROUP - 1

FLOPS = 2 * ROWS * (K + H) * GATES


def tile_multiinputlstmcell_pa_t_kernel(
    tc,
    input_,
    c_input,
    h_0,
    weight_ih,
    weight_hh,
    alpha_weight_ih,
    alpha_weight_hh,
    bias,
    alpha_bias,
    out_0,
    out_1,
):
    nc = tc.nc

    c_rows = c_input.rearrange("r o h -> r (o h)")

    with tc.tile_pool(name="consts", bufs=1) as consts, tc.tile_pool(
        name="two", bufs=2
    ) as two, tc.tile_pool(name="x_pool", bufs=3) as x_pool, tc.tile_pool(
        name="gates_pool", bufs=4
    ) as gates_pool, tc.tile_pool(name="pre_pool", bufs=LEAD + 2) as pre_pool, tc.psum_pool(
        name="psum", bufs=8
    ) as psum:
        warm = consts.tile([P, 1], F32)
        nc.vector.memset(warm[:], 0.0)
        nc.scalar.activation(out=warm[:], in_=warm[:], func=ACT.Sigmoid)

        whh = consts.tile([P, SIG], BF16)
        nc.scalar.dma_start(out=whh[:], in_=weight_hh)
        awhh = consts.tile([P, H], BF16)
        nc.scalar.dma_start(out=awhh[:], in_=alpha_weight_hh)

        bias_row = consts.tile([P, GATES], BF16)
        nc.vector.memset(bias_row[:], 0.0)
        nc.scalar.dma_start(out=bias_row[0:1, H:GATES], in_=bias.unsqueeze(0))
        nc.scalar.dma_start(out=bias_row[0:1, 0:H], in_=alpha_bias.unsqueeze(0))
        ones = consts.tile([P, P], BF16)
        nc.vector.memset(ones[:], 1.0)
        bias_all = consts.tile([P, GATES], F32)

        ident_f32 = consts.tile([P, P], F32)
        make_identity(nc, ident_f32[:])
        ident_bf = consts.tile([P, P], BF16)
        make_identity(nc, ident_bf[:])

        w_raw = consts.tile([P, PASSES, PACK, SIG], BF16)
        a_raw = consts.tile([P, PASSES, PACK, H], BF16)
        w_grouped = consts.tile([P, PASSES, GATES, PACK], BF16, align_bytes=64)
        w_codes = consts.tile([P, PASSES, GATES], U32, align_bytes=64)
        w_scales = consts.tile([P, PASSES, GATES], U8, align_bytes=64)
        h_sb = consts.tile([P, TILES * H], BF16)
        c_sb = consts.tile([P, TILES * H], BF16)

        def load_weights():
            for g in range(PASSES):
                k_rows = slice(g * K_PASS, (g + 1) * K_PASS)
                nc.sync.dma_start(
                    out=w_raw[:, g, :, :].rearrange("p (u e) c -> p u (e c)", e=2),
                    in_=weight_ih[k_rows, :].rearrange("(u p e) c -> p u (e c)", p=P, e=2),
                )
                nc.sync.dma_start(
                    out=a_raw[:, g, :, :].rearrange("p (u e) c -> p u (e c)", e=2),
                    in_=alpha_weight_ih[k_rows, :].rearrange("(u p e) c -> p u (e c)", p=P, e=2),
                )

        def regroup_weights():
            for g in range(PASSES):
                nc.vector.tensor_copy(
                    out=w_grouped[:, g, H:GATES, :],
                    in_=w_raw[:, g, :, :].rearrange("p t c -> p c t"),
                )
                nc.vector.tensor_copy(
                    out=w_grouped[:, g, 0:H, :],
                    in_=a_raw[:, g, :, :].rearrange("p t c -> p c t"),
                )

        def quantise_weights():
            for g in range(PASSES):
                nc.vector.quantize_mx(
                    out=w_codes[:, g, :].bitcast(FP8X4),
                    scales=w_scales[:, g, :],
                    in_=w_grouped[:, g, :, :].rearrange("p c t -> p (c t)"),
                )

        def spread_bias():
            bias_ps = psum.tile([P, GATES], F32, tag="bank")
            nc.tensor.matmul(bias_ps[:], lhsT=ones[:], rhs=bias_row[:], start=True, stop=True)
            nc.vector.tensor_copy(out=bias_all[:], in_=bias_ps[:])

        x_in, x_side, x_code, x_scale, hc_side = {}, {}, {}, {}, {}
        pre_of, gates_of, diff_of, w_of, move_of, c1_of, tanh_of, h1_of = {}, {}, {}, {}, {}, {}, {}, {}

        def rows_of(dram, grp):
            block, tile = FIRST[grp] // GROUP * GROUP * P, FIRST[grp] % GROUP
            rows = dram[block : block + GROUP * P, :].rearrange("(p n) w -> p n w", n=GROUP)
            return rows[:, tile : tile + SIZES[grp], :]

        def c_in_of(grp):
            lo = FIRST[grp] * H
            return c_sb[:, lo : lo + SIZES[grp] * H].rearrange("p (n h) -> p n h", h=H)


        def load_x(grp):
            x_sb = x_pool.tile([P, GROUP, K], BF16)
            nc.sync.dma_start(out=x_sb[:, 0 : SIZES[grp], :], in_=rows_of(input_, grp))
            x_in[grp] = x_sb

        def load_state(grp):
            lo = FIRST[grp]
            if lo > 0 and lo % (2 * GROUP) != GROUP:
                return
            n = GROUP
            tiles = slice(lo, min(lo + 2 * GROUP, TILES) if lo > 0 else GROUP)
            cols = slice(tiles.start * H, tiles.stop * H)
            for sb, dram in ((h_sb, h_0), (c_sb, c_rows)):
                nc.sync.dma_start(
                    out=sb[:, cols].rearrange("p (g w) -> p g w", w=n * H),
                    in_=dram[tiles.start * P : tiles.stop * P, :].rearrange("(g p n) h -> p g (n h)", p=P, n=n),
                )

        def transpose_state(grp):
            hc_ps = psum.tile([P, 2 * GROUP, P], BF16, tag="bank")
            n = SIZES[grp]
            for t in range(n):
                cols = slice((FIRST[grp] + t) * H, (FIRST[grp] + t + 1) * H)
                nc.tensor.transpose(hc_ps[:, t, :], h_sb[:, cols], ident_bf[:])
                nc.tensor.transpose(hc_ps[:, n + t, :], c_sb[:, cols], ident_bf[:])
            hc_t = x_pool.tile([P, 2 * GROUP, P], BF16)
            nc.scalar.copy(out=hc_t[:, 0 : 2 * n, :], in_=hc_ps[:, 0 : 2 * n, :])
            hc_side[grp] = hc_t

        def transpose_x(grp):
            x_words = x_in[grp][:].rearrange("p n k -> p (n k)").bitcast(F32)
            x_grouped = two.tile([P, GROUP * K], BF16, align_bytes=64)
            grouped_words = x_grouped[:].bitcast(F32)
            for t in range(SIZES[grp]):
                x_t = psum.tile([P, 2 * PASSES, P], F32, tag="bank")
                for j in range(2 * PASSES):
                    lo = t * WORDS + j * P
                    nc.tensor.transpose(x_t[:, j, :], x_words[:, lo : lo + P], ident_f32[:])
                nc.scalar.copy(
                    out=grouped_words[:, t * WORDS : (t + 1) * WORDS].rearrange(
                        "p (g r u) -> p g r u", g=PASSES, u=2
                    ),
                    in_=x_t[:].rearrange("p (g u) r -> p g r u", u=2),
                )
            x_side[grp] = x_grouped

        def quantise(grp):
            x_codes = two.tile([P, GROUP * PASSES * P], U32, align_bytes=64)
            x_scales = two.tile([P, GROUP * PASSES * P], U8, align_bytes=64)
            words = SIZES[grp] * PASSES * P
            nc.vector.quantize_mx(
                out=x_codes[:, 0:words].bitcast(FP8X4),
                scales=x_scales[:, 0:words],
                in_=x_side[grp][:, 0 : PACK * words],
            )
            x_code[grp] = x_codes
            x_scale[grp] = x_scales

        def plain_product(grp, t):
            if t == 0:
                pre = pre_pool.tile([P, GROUP, GATES], F32)
                pre_of[grp] = pre
            h_t = hc_side[grp][:, t, :]
            c_t = hc_side[grp][:, SIZES[grp] + t, :]
            plain = psum.tile([P, GATES], F32, tag="bank")
            by_scalar = grp < EARLY or t == SCALAR_TILE
            if by_scalar:
                nc.tensor.matmul(plain[:], lhsT=ones[:], rhs=bias_row[:], start=True, stop=False)
            nc.tensor.matmul(
                plain[:, H:GATES], lhsT=h_t, rhs=whh[:], start=not by_scalar, stop=not by_scalar
            )
            nc.tensor.matmul(plain[:, 0:H], lhsT=c_t, rhs=awhh[:], start=not by_scalar, stop=True)
            if by_scalar:
                nc.scalar.copy(out=pre_of[grp][:, t, :], in_=plain[:])
            else:
                nc.vector.tensor_tensor(out=pre_of[grp][:, t, :], in0=plain[:], in1=bias_all[:], op=ALU.add)

        def mx_product(grp, t):
            acc = psum.tile([P, GATES], F32, tag="bank")
            for g in range(PASSES):
                lo = (t * PASSES + g) * P
                nc.tensor.matmul_mx(
                    out=acc[:],
                    lhsT=x_code[grp][:, lo : lo + P].bitcast(FP8X4),
                    lhsT_scale=x_scale[grp][:, lo : lo + P],
                    rhs=w_codes[:, g, :].bitcast(FP8X4),
                    rhs_scale=w_scales[:, g, :],
                    start=(g == 0),
                    stop=(g == PASSES - 1),
                )
            pre_t = pre_of[grp][:, t, :]
            nc.vector.tensor_tensor(out=pre_t, in0=acc[:], in1=pre_t, op=ALU.add)

        def activate(grp):
            gates = gates_pool.tile([P, GROUP, GATES], F32)
            gates_of[grp] = gates[:, 0 : SIZES[grp], :]
            pre = pre_of[grp][:, 0 : SIZES[grp], :]
            nc.scalar.activation(out=gates_of[grp][:, :, 0:SIG], in_=pre[:, :, 0:SIG], func=ACT.Sigmoid)
            nc.scalar.activation(out=gates_of[grp][:, :, SIG:GATES], in_=pre[:, :, SIG:GATES], func=ACT.Tanh)

        def gate_difference(grp):
            gates = gates_of[grp]
            diff = two.tile([P, GROUP, H], F32)
            diff_of[grp] = diff[:, 0 : SIZES[grp], :]
            nc.vector.tensor_tensor(
                out=diff_of[grp], in0=gates[:, :, H : 2 * H], in1=gates[:, :, 0:H], op=ALU.subtract
            )

        def pair_weight(grp):
            w_i = two.tile([P, GROUP, H], F32)
            w_of[grp] = w_i[:, 0 : SIZES[grp], :]
            nc.scalar.activation(out=w_of[grp], in_=diff_of[grp], func=ACT.Sigmoid)

        def g_minus_c(grp):
            move = two.tile([P, GROUP, H], F32)
            move_of[grp] = move[:, 0 : SIZES[grp], :]
            nc.vector.tensor_tensor(
                out=move_of[grp], in0=gates_of[grp][:, :, SIG:GATES], in1=c_in_of(grp), op=ALU.subtract
            )

        def new_cell(grp, engine):
            step = two.tile([P, GROUP, H], F32)
            step = step[:, 0 : SIZES[grp], :]
            engine.tensor_tensor(out=step, in0=w_of[grp], in1=move_of[grp], op=ALU.mult)
            c_1 = gates_pool.tile([P, GROUP, H], F32)
            c1_of[grp] = c_1[:, 0 : SIZES[grp], :]
            engine.tensor_tensor(out=c1_of[grp], in0=step, in1=c_in_of(grp), op=ALU.add)
            nc.sync.dma_start(out=rows_of(out_1, grp), in_=c1_of[grp])

        def tanh_cell(grp):
            tanh_c = two.tile([P, GROUP, H], F32)
            tanh_of[grp] = tanh_c[:, 0 : SIZES[grp], :]
            nc.scalar.activation(out=tanh_of[grp], in_=c1_of[grp], func=ACT.Tanh)

        def new_hidden(grp, engine, lo, hi):
            hi = min(hi, SIZES[grp])
            if lo >= hi:
                return
            if lo == 0:
                h_1 = gates_pool.tile([P, GROUP, H], F32)
                h1_of[grp] = h_1
            engine.tensor_tensor(
                out=h1_of[grp][:, lo:hi, :],
                in0=gates_of[grp][:, lo:hi, 2 * H : SIG],
                in1=tanh_of[grp][:, lo:hi, :],
                op=ALU.mult,
            )
            if hi == SIZES[grp]:
                nc.sync.dma_start(out=rows_of(out_0, grp), in_=h1_of[grp][:, 0:hi, :])

        def run(stage, grp, *more):
            if 0 <= grp < N_GROUPS:
                stage(grp, *more)

        def run_tile(stage, grp, t):
            if 0 <= grp < N_GROUPS and t < SIZES[grp]:
                stage(grp, t)

        with tc.manual_schedule():
            for rnd in range(-LEAD - 3, N_GROUPS + 3):
                if rnd == -LEAD - 3:
                    load_weights()
                run(load_x, rnd + 3)
                run(load_state, rnd + LEAD + 3)
                run(activate, rnd - 1)
                if rnd + LEAD == 0:
                    spread_bias()
                for pair in range(0, GROUP, 2):
                    for t in (pair, pair + 1):
                        run_tile(plain_product, rnd + LEAD, t)
                    for t in (pair, pair + 1):
                        run_tile(mx_product, rnd, t)
                run(transpose_x, rnd + 2)
                if rnd + LEAD + 2 == 0:
                    regroup_weights()
                    quantise_weights()
                if rnd - 2 >= CELL_BY_VECTOR:
                    run(new_cell, rnd - 2, nc.vector)
                run(gate_difference, rnd - 1)
                run(quantise, rnd + 1)
                run(g_minus_c, rnd - 1)
                if rnd - 3 < HIDDEN_BY_VECTOR:
                    run(new_hidden, rnd - 3, nc.vector, 0, GROUP // 2)
                run(pair_weight, rnd - 1)
                run(transpose_state, rnd + LEAD + 2)
                if rnd - 1 < CELL_BY_VECTOR:
                    run(new_cell, rnd - 1, nc.gpsimd)
                run(tanh_cell, rnd - 2)
                if rnd - 3 < HIDDEN_BY_VECTOR:
                    run(new_hidden, rnd - 3, nc.gpsimd, GROUP // 2, GROUP)
                else:
                    run(new_hidden, rnd - 3, nc.vector, 0, GROUP)
